import numpy as np
import ml_dtypes


def mxq(x, axis, fmt="e4m3"):
    dtype, down = {"e4m3": (ml_dtypes.float8_e4m3fn, 7), "e5m2": (ml_dtypes.float8_e5m2, 14)}[fmt]
    v = np.moveaxis(np.asarray(x, np.float32).astype(ml_dtypes.bfloat16).astype(np.float64), axis, -1)
    blocks = v.reshape(v.shape[:-1] + (-1, 32))
    amax = np.abs(blocks).max(-1, keepdims=True)
    byte = np.maximum(np.where(amax > 0, np.frexp(amax)[1] - 1 + 127, 0) - down, 1)
    scale = np.exp2(byte - 127.0)
    codes = (blocks / scale).astype(np.float32).astype(dtype).astype(np.float64)
    return np.moveaxis((codes * scale).reshape(v.shape), -1, axis)


WIDE = False


def mx_kscale(k):
    if not WIDE:
        return np.ones(k)
    levels = np.array([10, -10, 5, -5, 0])
    a = np.random.permutation(np.resize(levels, k // 512 * 4)).reshape(k // 512, 4)
    idx = np.arange(k)
    return np.exp2(a[idx // 512, idx % 128 // 32])


BF16 = ml_dtypes.bfloat16


def bf(x):
    return np.asarray(x, np.float32).astype(BF16)


def f64(x):
    return np.asarray(x).astype(np.float64)


B, D_IN, D_FEAT, N_EX, N_LAB = 8192, 512, 1024, 512, 128
P_FACTOR = 3.0
EPS = 1e-12


def unit_rows(x):
    return x / np.sqrt((x * x).sum(-1, keepdims=True))


def l1_normalize(x):
    n = np.abs(x).sum(-1, keepdims=True)
    return x / np.maximum(n, EPS)


def setup_inputs():
    s = mx_kscale(D_FEAT)
    return {"f_norm": bf(unit_rows(np.random.standard_normal((B, D_FEAT))) * s),
            "e_norm": bf(unit_rows(np.random.standard_normal((N_EX, D_FEAT))) / s),
            "ex_class_reps": bf(np.random.standard_normal((N_EX, N_LAB)) * 0.0625 * np.sqrt(N_EX))}


def reference(f_norm, e_norm, ex_class_reps):
    s = mxq(f64(f_norm), 1, "e4m3") @ mxq(f64(e_norm), 1, "e4m3").T
    a = np.sign(s) * np.abs(s) ** P_FACTOR
    a = l1_normalize(a)
    return mxq(a, 1, "e4m3") @ mxq(f64(ex_class_reps), 0, "e4m3")

@@ -1,0 +1,218 @@
+from contextlib import ExitStack
+
+import concourse.bass as bass
+import concourse.mybir as mybir
+import concourse.tile as tile
+from concourse.masks import make_identity
+
+F32 = mybir.dt.float32
+BF16 = mybir.dt.bfloat16
+U32 = mybir.dt.uint32
+U8 = mybir.dt.uint8
+FP8X4 = mybir.dt.float8_e4m3fn_x4
+ALU = mybir.AluOpType
+ACTF = mybir.ActivationFunctionType
+
+P = 128
+B, D_FEAT, N_EX, N_LAB = 8192, 1024, 512, 128
+EPS = 1e-12
+FLOPS = 2 * B * D_FEAT * N_EX + 2 * B * N_EX * N_LAB
+
+CHUNK_TILES = 4
+N_CHUNKS = B // (P * CHUNK_TILES)
+GT = 2
+NG = B // (P * GT)
+PIN = True
+
+
+def tile_minerva_pa_t_kernel(tc, f_norm, e_norm, ex_class_reps, out):
+    nc = tc.nc
+    with ExitStack() as ctx:
+        const = ctx.enter_context(tc.tile_pool(name="const", bufs=1))
+        loads = ctx.enter_context(tc.tile_pool(name="loads", bufs=N_CHUNKS))
+        work = ctx.enter_context(tc.tile_pool(name="work", bufs=2))
+        psum = ctx.enter_context(tc.psum_pool(name="psum", bufs=1))
+        if PIN:
+            ctx.enter_context(tc.manual_schedule())
+
+        ident_f = const.tile([P, P], F32)
+        make_identity(nc, ident_f[:])
+        ident_b = const.tile([P, P], BF16)
+        make_identity(nc, ident_b[:])
+
+        es = const.tile([P, 4 * D_FEAT], BF16)
+        nc.sync.dma_start(out=es[:], in_=e_norm.rearrange("(p j) k -> p (j k)", j=4))
+        fs = []
+        for c in range(N_CHUNKS):
+            fs_c = loads.tile([P, CHUNK_TILES * D_FEAT], BF16, tag="fs", name="fs_c")
+            fs.append(fs_c)
+        rs = const.tile([P, 4, N_LAB], BF16)
+
+        def load_f(c):
+            rows = f_norm[c * P * CHUNK_TILES : (c + 1) * P * CHUNK_TILES, :]
+            nc.sync.dma_start(out=fs[c][:], in_=rows.rearrange("(p t) k -> p (t k)", t=CHUNK_TILES))
+
+        load_f(0)
+        nc.sync.dma_start(out=rs[:], in_=ex_class_reps.rearrange("(q t) l -> q t l", t=4))
+        for c in range(1, N_CHUNKS):
+            load_f(c)
+
+        def word_transposes(dst, words):
+            for g in range(2):
+                for u in range(2):
+                    lo = 256 * g + 128 * u
+                    nc.tensor.transpose(dst[:, g, u, :], words[:, lo : lo + P], ident_f[:])
+
+        eg = const.tile([P, 4 * 2 * N_EX], BF16, align_bytes=64)
+        egw = eg[:].bitcast(F32).rearrange("p (g j b u) -> p g j b u", g=2, j=4, b=P, u=2)
+        ec = const.tile([P, 2 * N_EX], U32, align_bytes=64)
+        esc = const.tile([P, 2 * N_EX], U8, align_bytes=64)
+        esw = es[:].bitcast(F32)
+        for j in range(4):
+            et = psum.tile([P, 2, 2, P], F32, tag="ft", bufs=2, name="et")
+            word_transposes(et, esw[:, 512 * j : 512 * (j + 1)])
+            src = et[:].rearrange("p g u b -> p g b u")
+            if j % 2 == 0:
+                nc.scalar.copy(out=egw[:, :, j, :, :], in_=src)
+            else:
+                nc.vector.tensor_copy(out=egw[:, :, j, :, :], in_=src)
+        for g in range(2):
+            nc.vector.quantize_mx(
+                out=ec[:, g * N_EX : (g + 1) * N_EX].bitcast(FP8X4),
+                scales=esc[:, g * N_EX : (g + 1) * N_EX],
+                in_=eg[:, g * 4 * N_EX : (g + 1) * 4 * N_EX],
+            )
+
+        rg = const.tile([P, N_LAB, 4], BF16, align_bytes=64)
+        nc.vector.tensor_copy(out=rg[:], in_=rs[:].rearrange("q t l -> q l t"))
+        rc = const.tile([P, N_LAB], U32, align_bytes=64)
+        rsc = const.tile([P, N_LAB], U8, align_bytes=64)
+        nc.vector.quantize_mx(out=rc[:].bitcast(FP8X4), scales=rsc[:], in_=rg[:].rearrange("q l t -> q (l t)"))
+
+        st = {}
+
+        def ok(g):
+            return 0 <= g < NG
+
+        def t_f(g):
+            for j in range(GT):
+                t = g * GT + j
+                ft = psum.tile([P, 2, 2, P], F32, tag="ft", bufs=2, name="ft")
+                words = fs[t // CHUNK_TILES][:].bitcast(F32)
+                lo = 512 * (t % CHUNK_TILES)
+                word_transposes(ft, words[:, lo : lo + 512])
+                st[("ft", g, j)] = ft
+
+        def op_a(g):
+            fg = work.tile([P, GT * 2 * P * 4], BF16, tag="fg", bufs=2, align_bytes=64, name="fg")
+            fgw = fg[:].bitcast(F32).rearrange("p (j g b u) -> p j g b u", j=GT, g=2, b=P, u=2)
+            for j in range(GT):
+                nc.scalar.copy(out=fgw[:, j], in_=st[("ft", g, j)][:].rearrange("p g u b -> p g b u"))
+            st[("fg", g)] = fg
+
+        def op_b(g):
+            fc = work.tile([P, GT * 2 * P], U32, tag="fc", bufs=3, align_bytes=64, name="fc")
+            fsc = work.tile([P, GT * 2 * P], U8, tag="fsc", bufs=3, align_bytes=64, name="fsc")
+            nc.vector.quantize_mx(out=fc[:].bitcast(FP8X4), scales=fsc[:], in_=st[("fg", g)][:])
+            st[("fc", g)] = (fc, fsc)
+
+        def mm1(g):
+            fc, fsc = st[("fc", g)]
+            for j in range(GT):
+                s = psum.tile([P, N_EX], F32, tag="s", bufs=4, name="s")
+                for h in range(2):
+                    lo = (j * 2 + h) * P
+                    nc.tensor.matmul_mx(
+                        out=s[:],
+                        lhsT=fc[:, lo : lo + P].bitcast(FP8X4),
+                        lhsT_scale=fsc[:, lo : lo + P],
+                        rhs=ec[:, h * N_EX : (h + 1) * N_EX].bitcast(FP8X4),
+                        rhs_scale=esc[:, h * N_EX : (h + 1) * N_EX],
+                        start=(h == 0),
+                        stop=(h == 1),
+                    )
+                st[("s", g, j)] = s
+
+        def op_c(g):
+            for j in range(GT):
+                s2 = work.tile([P, N_EX], F32, tag="s2", bufs=4, name="s2")
+                nc.scalar.activation(out=s2[:], in_=st[("s", g, j)][:], func=ACTF.Square)
+                st[("s2", g, j)] = s2
+
+        def op_d(g):
+            for j in range(GT):
+                a = work.tile([P, N_EX], F32, tag="a", bufs=6, name="a")
+                nc.vector.tensor_tensor(out=a[:], in0=st[("s", g, j)][:], in1=st[("s2", g, j)][:], op=ALU.mult)
+                st[("a", g, j)] = a
+
+        def op_e(g):
+            sums = work.tile([P, GT], F32, tag="sums", bufs=3, name="sums")
+            for j in range(GT):
+                junk = work.tile([P, N_EX], BF16, tag="junk", bufs=2, name="junk")
+                nc.scalar.activation(out=junk[:], in_=st[("a", g, j)][:], func=ACTF.Abs, accum_out=sums[:, j : j + 1])
+            st[("sums", g)] = sums
+
+        def op_fg(g):
+            floor = work.tile([P, GT], F32, tag="floor", bufs=2, name="floor")
+            nc.vector.tensor_scalar_max(out=floor[:], in0=st[("sums", g)][:], scalar1=EPS)
+            rin = work.tile([P, GT], F32, tag="rin", bufs=2, name="rin")
+            nc.vector.reciprocal(out=rin[:], in_=floor[:])
+            p = work.tile([P, GT, N_EX], BF16, tag="p", bufs=3, name="p")
+            for j in range(GT):
+                nc.vector.tensor_scalar(
+                    out=p[:, j, :], in0=st[("a", g, j)][:], scalar1=rin[:, j : j + 1], scalar2=None, op0=ALU.mult
+                )
+            st[("p", g)] = p
+
+        def t_p(g):
+            p = st[("p", g)]
+            pt = psum.tile([P, GT, 4, P], BF16, tag="pt", bufs=1, name="pt")
+            for j in range(GT):
+                for t in range(4):
+                    nc.tensor.transpose(pt[:, j, t, :], p[:, j, t * P : (t + 1) * P], ident_b[:])
+            st[("pt", g)] = pt
+
+        def op_h(g):
+            pg = work.tile([P, GT, P, 4], BF16, tag="pg", bufs=2, align_bytes=64, name="pg")
+            nc.vector.tensor_copy(out=pg[:], in_=st[("pt", g)][:].rearrange("p j t b -> p j b t"))
+            st[("pg", g)] = pg
+
+        def op_i(g):
+            pc = work.tile([P, GT * P], U32, tag="pc", bufs=2, align_bytes=64, name="pc")
+            psc = work.tile([P, GT * P], U8, tag="psc", bufs=2, align_bytes=64, name="psc")
+            nc.vector.quantize_mx(
+                out=pc[:].bitcast(FP8X4), scales=psc[:], in_=st[("pg", g)][:].rearrange("p j b t -> p (j b t)")
+            )
+            st[("pc", g)] = (pc, psc)
+
+        def mm2(g):
+            pc, psc = st[("pc", g)]
+            o = psum.tile([P, GT, N_LAB], F32, tag="o", bufs=1, name="o")
+            for j in range(GT):
+                nc.tensor.matmul_mx(
+                    out=o[:, j, :],
+                    lhsT=pc[:, j * P : (j + 1) * P].bitcast(FP8X4),
+                    lhsT_scale=psc[:, j * P : (j + 1) * P],
+                    rhs=rc[:].bitcast(FP8X4),
+                    rhs_scale=rsc[:],
+                    start=True,
+                    stop=True,
+                )
+            st[("o", g)] = o
+
+        def op_j(g):
+            osb = work.tile([P, GT, N_LAB], F32, tag="osb", bufs=3, name="osb")
+            nc.scalar.copy(out=osb[:], in_=st[("o", g)][:])
+            c = (g * GT) // CHUNK_TILES
+            t0 = (g * GT) % CHUNK_TILES
+            rows = out[c * P * CHUNK_TILES : (c + 1) * P * CHUNK_TILES, :].rearrange("(p t) l -> p t l", t=CHUNK_TILES)
+            nc.sync.dma_start(out=rows[:, t0 : t0 + GT, :], in_=osb[:])
+
+        plan = (
+            (mm2, -2), (mm1, 1), (op_c, 0), (op_fg, -1), (t_p, -1), (op_a, 2), (t_f, 3),
+            (op_d, 0), (op_e, 0), (op_h, -1), (op_b, 2), (op_i, -1), (op_j, -2),
+        )
+        for i in range(-3, NG + 2):
+            for fn, d in plan:
+                if ok(i + d):
+                    fn(i + d)

@@ -141,7 +141,7 @@ def tile_minerva_pa_t_kernel(tc, f_norm, e_norm, ex_class_reps, out):
 
         def op_d(g):
             for j in range(GT):
-                a = work.tile([P, N_EX], F32, tag="a", bufs=6, name="a")
+                a = work.tile([P, N_EX], F32, tag="a", bufs=8, name="a")
                 nc.vector.tensor_tensor(out=a[:], in0=st[("s", g, j)][:], in1=st[("s2", g, j)][:], op=ALU.mult)
                 st[("a", g, j)] = a
 
@@ -209,10 +209,10 @@ def tile_minerva_pa_t_kernel(tc, f_norm, e_norm, ex_class_reps, out):
             nc.sync.dma_start(out=rows[:, t0 : t0 + GT, :], in_=osb[:])
 
         plan = (
-            (mm2, -2), (mm1, 1), (op_c, 0), (op_fg, -1), (t_p, -1), (op_a, 2), (t_f, 3),
-            (op_d, 0), (op_e, 0), (op_h, -1), (op_b, 2), (op_i, -1), (op_j, -2),
+            (op_a, 1), (op_fg, -2), (mm2, -4), (op_h, -3), (op_c, 0), (t_f, 2), (op_b, 1),
+            (op_e, -1), (t_p, -2), (op_d, 0), (mm1, 1), (op_j, -4), (op_i, -3),
         )
-        for i in range(-3, NG + 2):
+        for i in range(-2, NG + 4):
             for fn, d in plan:
                 if ok(i + d):
                     fn(i + d)

@@ -41,21 +41,27 @@ def tile_minerva_pa_t_kernel(tc, f_norm, e_norm, ex_class_reps, out):
         make_identity(nc, ident_b[:])
 
         es = const.tile([P, 4 * D_FEAT], BF16)
-        nc.sync.dma_start(out=es[:], in_=e_norm.rearrange("(p j) k -> p (j k)", j=4))
+        e_rows = e_norm.rearrange("(p j) k -> p j k", j=4)
         fs = []
         for c in range(N_CHUNKS):
             fs_c = loads.tile([P, CHUNK_TILES * D_FEAT], BF16, tag="fs", name="fs_c")
             fs.append(fs_c)
         rs = const.tile([P, 4, N_LAB], BF16)
 
-        def load_f(c):
+        def load_f(c, lo, hi):
             rows = f_norm[c * P * CHUNK_TILES : (c + 1) * P * CHUNK_TILES, :]
-            nc.sync.dma_start(out=fs[c][:], in_=rows.rearrange("(p t) k -> p (t k)", t=CHUNK_TILES))
+            nc.sync.dma_start(
+                out=fs[c][:, lo * D_FEAT : hi * D_FEAT],
+                in_=rows.rearrange("(p t) k -> p t k", t=CHUNK_TILES)[:, lo:hi, :].rearrange("p t k -> p (t k)"),
+            )
 
-        load_f(0)
+        load_f(0, 0, GT)
+        for j in range(4):
+            nc.sync.dma_start(out=es[:, j * D_FEAT : (j + 1) * D_FEAT], in_=e_rows[:, j, :])
+        load_f(0, GT, CHUNK_TILES)
         nc.sync.dma_start(out=rs[:], in_=ex_class_reps.rearrange("(q t) l -> q t l", t=4))
         for c in range(1, N_CHUNKS):
-            load_f(c)
+            load_f(c, 0, CHUNK_TILES)
 
         def word_transposes(dst, words):
             for g in range(2):
@@ -68,26 +74,32 @@ def tile_minerva_pa_t_kernel(tc, f_norm, e_norm, ex_class_reps, out):
         ec = const.tile([P, 2 * N_EX], U32, align_bytes=64)
         esc = const.tile([P, 2 * N_EX], U8, align_bytes=64)
         esw = es[:].bitcast(F32)
-        for j in range(4):
-            et = psum.tile([P, 2, 2, P], F32, tag="ft", bufs=2, name="et")
-            word_transposes(et, esw[:, 512 * j : 512 * (j + 1)])
-            src = et[:].rearrange("p g u b -> p g b u")
-            if j % 2 == 0:
-                nc.scalar.copy(out=egw[:, :, j, :, :], in_=src)
-            else:
-                nc.vector.tensor_copy(out=egw[:, :, j, :, :], in_=src)
-        for g in range(2):
-            nc.vector.quantize_mx(
-                out=ec[:, g * N_EX : (g + 1) * N_EX].bitcast(FP8X4),
-                scales=esc[:, g * N_EX : (g + 1) * N_EX],
-                in_=eg[:, g * 4 * N_EX : (g + 1) * 4 * N_EX],
-            )
+
+        def e_transpose():
+            for j in range(4):
+                et = psum.tile([P, 2, 2, P], F32, tag="s", bufs=4, name="et")
+                word_transposes(et, esw[:, 512 * j : 512 * (j + 1)])
+                src = et[:].rearrange("p g u b -> p g b u")
+                if j % 2 == 0:
+                    nc.scalar.copy(out=egw[:, :, j, :, :], in_=src)
+                else:
+                    nc.vector.tensor_copy(out=egw[:, :, j, :, :], in_=src)
+
+        def e_quantise():
+            for g in range(2):
+                nc.vector.quantize_mx(
+                    out=ec[:, g * N_EX : (g + 1) * N_EX].bitcast(FP8X4),
+                    scales=esc[:, g * N_EX : (g + 1) * N_EX],
+                    in_=eg[:, g * 4 * N_EX : (g + 1) * 4 * N_EX],
+                )
 
         rg = const.tile([P, N_LAB, 4], BF16, align_bytes=64)
-        nc.vector.tensor_copy(out=rg[:], in_=rs[:].rearrange("q t l -> q l t"))
         rc = const.tile([P, N_LAB], U32, align_bytes=64)
         rsc = const.tile([P, N_LAB], U8, align_bytes=64)
-        nc.vector.quantize_mx(out=rc[:].bitcast(FP8X4), scales=rsc[:], in_=rg[:].rearrange("q l t -> q (l t)"))
+
+        def r_prep():
+            nc.vector.tensor_copy(out=rg[:], in_=rs[:].rearrange("q t l -> q l t"))
+            nc.vector.quantize_mx(out=rc[:].bitcast(FP8X4), scales=rsc[:], in_=rg[:].rearrange("q l t -> q (l t)"))
 
         st = {}
 
@@ -104,7 +116,7 @@ def tile_minerva_pa_t_kernel(tc, f_norm, e_norm, ex_class_reps, out):
                 st[("ft", g, j)] = ft
 
         def op_a(g):
-            fg = work.tile([P, GT * 2 * P * 4], BF16, tag="fg", bufs=2, align_bytes=64, name="fg")
+            fg = work.tile([P, GT * 2 * P * 4], BF16, tag="fg", bufs=3, align_bytes=64, name="fg")
             fgw = fg[:].bitcast(F32).rearrange("p (j g b u) -> p j g b u", j=GT, g=2, b=P, u=2)
             for j in range(GT):
                 nc.scalar.copy(out=fgw[:, j], in_=st[("ft", g, j)][:].rearrange("p g u b -> p g b u"))
@@ -141,26 +153,34 @@ def tile_minerva_pa_t_kernel(tc, f_norm, e_norm, ex_class_reps, out):
 
         def op_d(g):
             for j in range(GT):
-                a = work.tile([P, N_EX], F32, tag="a", bufs=8, name="a")
+                a = work.tile([P, N_EX], F32, tag="a", bufs=10, name="a")
                 nc.vector.tensor_tensor(out=a[:], in0=st[("s", g, j)][:], in1=st[("s2", g, j)][:], op=ALU.mult)
                 st[("a", g, j)] = a
 
         def op_e(g):
-            sums = work.tile([P, GT], F32, tag="sums", bufs=3, name="sums")
+            sums = work.tile([P, GT], F32, tag="sums", bufs=4, name="sums")
             for j in range(GT):
                 junk = work.tile([P, N_EX], BF16, tag="junk", bufs=2, name="junk")
                 nc.scalar.activation(out=junk[:], in_=st[("a", g, j)][:], func=ACTF.Abs, accum_out=sums[:, j : j + 1])
             st[("sums", g)] = sums
 
-        def op_fg(g):
+        def op_f1(g):
             floor = work.tile([P, GT], F32, tag="floor", bufs=2, name="floor")
             nc.vector.tensor_scalar_max(out=floor[:], in0=st[("sums", g)][:], scalar1=EPS)
-            rin = work.tile([P, GT], F32, tag="rin", bufs=2, name="rin")
-            nc.vector.reciprocal(out=rin[:], in_=floor[:])
+            st[("floor", g)] = floor
+
+        def op_f2(g):
+            rin = work.tile([P, GT], F32, tag="rin", bufs=3, name="rin")
+            nc.vector.reciprocal(out=rin[:], in_=st[("floor", g)][:])
+            st[("rin", g)] = rin
+
+        def op_g(g):
+            rin = st[("rin", g)]
             p = work.tile([P, GT, N_EX], BF16, tag="p", bufs=3, name="p")
             for j in range(GT):
-                nc.vector.tensor_scalar(
-                    out=p[:, j, :], in0=st[("a", g, j)][:], scalar1=rin[:, j : j + 1], scalar2=None, op0=ALU.mult
+                nc.gpsimd.tensor_scalar(
+                    out=p[:, j, :], in0=st[("a", g, j)][:], scalar1=rin[:, j : j + 1], scalar2=0.0,
+                    op0=ALU.mult, op1=ALU.add,
                 )
             st[("p", g)] = p
 
@@ -202,17 +222,24 @@ def tile_minerva_pa_t_kernel(tc, f_norm, e_norm, ex_class_reps, out):
 
         def op_j(g):
             osb = work.tile([P, GT, N_LAB], F32, tag="osb", bufs=3, name="osb")
-            nc.scalar.copy(out=osb[:], in_=st[("o", g)][:])
+            nc.vector.tensor_copy(out=osb[:], in_=st[("o", g)][:])
             c = (g * GT) // CHUNK_TILES
             t0 = (g * GT) % CHUNK_TILES
             rows = out[c * P * CHUNK_TILES : (c + 1) * P * CHUNK_TILES, :].rearrange("(p t) l -> p t l", t=CHUNK_TILES)
             nc.sync.dma_start(out=rows[:, t0 : t0 + GT, :], in_=osb[:])
 
         plan = (
-            (op_a, 1), (op_fg, -2), (mm2, -4), (op_h, -3), (op_c, 0), (t_f, 2), (op_b, 1),
-            (op_e, -1), (t_p, -2), (op_d, 0), (mm1, 1), (op_j, -4), (op_i, -3),
+            (op_c, 0), (op_f1, -3), (op_h, -5), (mm1, 1), (op_a, 3), (op_j, -6), (op_f2, -3), (op_b, 2),
+            (op_i, -5), (t_p, -4), (op_g, -3), (op_d, 0), (op_e, -1), (t_f, 4), (mm2, -5),
         )
-        for i in range(-2, NG + 4):
+        t_f(0)
+        op_a(0)
+        e_transpose()
+        op_b(0)
+        e_quantise()
+        r_prep()
+        early = ((t_f, 0), (op_a, 0), (op_b, 0))
+        for i in range(-4, NG + 6):
             for fn, d in plan:
-                if ok(i + d):
+                if ok(i + d) and (fn, i + d) not in early:
                     fn(i + d)

@@ -23,6 +23,8 @@ N_CHUNKS = B // (P * CHUNK_TILES)
 GT = 2
 NG = B // (P * GT)
 PIN = True
+TAIL_G = NG - 1
+TAIL_BANKS = NG - 3
 
 
 def tile_minerva_pa_t_kernel(tc, f_norm, e_norm, ex_class_reps, out):
@@ -39,6 +41,8 @@ def tile_minerva_pa_t_kernel(tc, f_norm, e_norm, ex_class_reps, out):
         make_identity(nc, ident_f[:])
         ident_b = const.tile([P, P], BF16)
         make_identity(nc, ident_b[:])
+        neg1 = const.tile([P, GT], F32)
+        nc.gpsimd.memset(neg1[:], -1.0)
 
         es = const.tile([P, 4 * D_FEAT], BF16)
         e_rows = e_norm.rearrange("(p j) k -> p j k", j=4)
@@ -153,7 +157,7 @@ def tile_minerva_pa_t_kernel(tc, f_norm, e_norm, ex_class_reps, out):
 
         def op_d(g):
             for j in range(GT):
-                a = work.tile([P, N_EX], F32, tag="a", bufs=10, name="a")
+                a = work.tile([P, N_EX], F32, tag="a", bufs=8, name="a")
                 nc.vector.tensor_tensor(out=a[:], in0=st[("s", g, j)][:], in1=st[("s2", g, j)][:], op=ALU.mult)
                 st[("a", g, j)] = a
 
@@ -166,27 +170,41 @@ def tile_minerva_pa_t_kernel(tc, f_norm, e_norm, ex_class_reps, out):
 
         def op_f1(g):
             floor = work.tile([P, GT], F32, tag="floor", bufs=2, name="floor")
-            nc.vector.tensor_scalar_max(out=floor[:], in0=st[("sums", g)][:], scalar1=EPS)
+            if g < TAIL_G:
+                nc.gpsimd.tensor_scalar_max(out=floor[:], in0=st[("sums", g)][:], scalar1=EPS)
+            else:
+                nc.vector.tensor_scalar_max(out=floor[:], in0=st[("sums", g)][:], scalar1=EPS)
             st[("floor", g)] = floor
 
         def op_f2(g):
             rin = work.tile([P, GT], F32, tag="rin", bufs=3, name="rin")
-            nc.vector.reciprocal(out=rin[:], in_=st[("floor", g)][:])
+            if g < TAIL_G:
+                nc.gpsimd.tensor_tensor(out=rin[:], in0=st[("floor", g)][:], in1=neg1[:], op=ALU.pow)
+            else:
+                nc.vector.reciprocal(out=rin[:], in_=st[("floor", g)][:])
             st[("rin", g)] = rin
 
         def op_g(g):
             rin = st[("rin", g)]
             p = work.tile([P, GT, N_EX], BF16, tag="p", bufs=3, name="p")
             for j in range(GT):
-                nc.gpsimd.tensor_scalar(
-                    out=p[:, j, :], in0=st[("a", g, j)][:], scalar1=rin[:, j : j + 1], scalar2=0.0,
-                    op0=ALU.mult, op1=ALU.add,
-                )
+                if g < TAIL_G:
+                    nc.gpsimd.tensor_scalar(
+                        out=p[:, j, :], in0=st[("a", g, j)][:], scalar1=rin[:, j : j + 1], scalar2=0.0,
+                        op0=ALU.mult, op1=ALU.add,
+                    )
+                else:
+                    nc.vector.tensor_scalar(
+                        out=p[:, j, :], in0=st[("a", g, j)][:], scalar1=rin[:, j : j + 1], scalar2=None, op0=ALU.mult
+                    )
             st[("p", g)] = p
 
         def t_p(g):
             p = st[("p", g)]
-            pt = psum.tile([P, GT, 4, P], BF16, tag="pt", bufs=1, name="pt")
+            if g < TAIL_BANKS:
+                pt = psum.tile([P, GT, 4, P], BF16, tag="pt", bufs=1, name="pt")
+            else:
+                pt = psum.tile([P, GT, 4, P], BF16, tag="s", bufs=4, name="pt")
             for j in range(GT):
                 for t in range(4):
                     nc.tensor.transpose(pt[:, j, t, :], p[:, j, t * P : (t + 1) * P], ident_b[:])
@@ -207,7 +225,10 @@ def tile_minerva_pa_t_kernel(tc, f_norm, e_norm, ex_class_reps, out):
 
         def mm2(g):
             pc, psc = st[("pc", g)]
-            o = psum.tile([P, GT, N_LAB], F32, tag="o", bufs=1, name="o")
+            if g < TAIL_BANKS:
+                o = psum.tile([P, GT, N_LAB], F32, tag="o", bufs=1, name="o")
+            else:
+                o = psum.tile([P, GT, N_LAB], F32, tag="ft", bufs=2, name="o")
             for j in range(GT):
                 nc.tensor.matmul_mx(
                     out=o[:, j, :],
@@ -229,8 +250,8 @@ def tile_minerva_pa_t_kernel(tc, f_norm, e_norm, ex_class_reps, out):
             nc.sync.dma_start(out=rows[:, t0 : t0 + GT, :], in_=osb[:])
 
         plan = (
-            (op_c, 0), (op_f1, -3), (op_h, -5), (mm1, 1), (op_a, 3), (op_j, -6), (op_f2, -3), (op_b, 2),
-            (op_i, -5), (t_p, -4), (op_g, -3), (op_d, 0), (op_e, -1), (t_f, 4), (mm2, -5),
+            (op_h, -4), (t_p, -3), (op_j, -5), (op_f1, -2), (op_f2, -2), (op_c, 0), (op_e, -1), (op_a, 3),
+            (op_i, -4), (op_b, 2), (mm2, -4), (mm1, 1), (op_g, -2), (op_d, 0), (t_f, 4),
         )
         t_f(0)
         op_a(0)
@@ -239,7 +260,7 @@ def tile_minerva_pa_t_kernel(tc, f_norm, e_norm, ex_class_reps, out):
         e_quantise()
         r_prep()
         early = ((t_f, 0), (op_a, 0), (op_b, 0))
-        for i in range(-4, NG + 6):
+        for i in range(-4, NG + 5):
             for fn, d in plan:
                 if ok(i + d) and (fn, i + d) not in early:
                     fn(i + d)

@@ -41,8 +41,6 @@ def tile_minerva_pa_t_kernel(tc, f_norm, e_norm, ex_class_reps, out):
         make_identity(nc, ident_f[:])
         ident_b = const.tile([P, P], BF16)
         make_identity(nc, ident_b[:])
-        neg1 = const.tile([P, GT], F32)
-        nc.gpsimd.memset(neg1[:], -1.0)
 
         es = const.tile([P, 4 * D_FEAT], BF16)
         e_rows = e_norm.rearrange("(p j) k -> p j k", j=4)
@@ -170,18 +168,12 @@ def tile_minerva_pa_t_kernel(tc, f_norm, e_norm, ex_class_reps, out):
 
         def op_f1(g):
             floor = work.tile([P, GT], F32, tag="floor", bufs=2, name="floor")
-            if g < TAIL_G:
-                nc.gpsimd.tensor_scalar_max(out=floor[:], in0=st[("sums", g)][:], scalar1=EPS)
-            else:
-                nc.vector.tensor_scalar_max(out=floor[:], in0=st[("sums", g)][:], scalar1=EPS)
+            nc.vector.tensor_scalar_max(out=floor[:], in0=st[("sums", g)][:], scalar1=EPS)
             st[("floor", g)] = floor
 
         def op_f2(g):
             rin = work.tile([P, GT], F32, tag="rin", bufs=3, name="rin")
-            if g < TAIL_G:
-                nc.gpsimd.tensor_tensor(out=rin[:], in0=st[("floor", g)][:], in1=neg1[:], op=ALU.pow)
-            else:
-                nc.vector.reciprocal(out=rin[:], in_=st[("floor", g)][:])
+            nc.vector.reciprocal(out=rin[:], in_=st[("floor", g)][:])
             st[("rin", g)] = rin
 
         def op_g(g):
@@ -250,8 +242,8 @@ def tile_minerva_pa_t_kernel(tc, f_norm, e_norm, ex_class_reps, out):
             nc.sync.dma_start(out=rows[:, t0 : t0 + GT, :], in_=osb[:])
 
         plan = (
-            (op_h, -4), (t_p, -3), (op_j, -5), (op_f1, -2), (op_f2, -2), (op_c, 0), (op_e, -1), (op_a, 3),
-            (op_i, -4), (op_b, 2), (mm2, -4), (mm1, 1), (op_g, -2), (op_d, 0), (t_f, 4),
+            (op_i, -5), (t_p, -4), (op_a, 2), (mm1, 0), (op_j, -6), (op_d, -1), (op_h, -4), (op_c, 0),
+            (mm2, -5), (op_f1, -2), (t_f, 3), (op_e, -1), (op_b, 2), (op_f2, -2), (op_g, -2),
         )
         t_f(0)
         op_a(0)
@@ -260,7 +252,7 @@ def tile_minerva_pa_t_kernel(tc, f_norm, e_norm, ex_class_reps, out):
         e_quantise()
         r_prep()
         early = ((t_f, 0), (op_a, 0), (op_b, 0))
-        for i in range(-4, NG + 5):
+        for i in range(-3, NG + 6):
             for fn, d in plan:
                 if ok(i + d) and (fn, i + d) not in early:
                     fn(i + d)

@@ -1,8 +1,6 @@
 from contextlib import ExitStack
 
-import concourse.bass as bass
 import concourse.mybir as mybir
-import concourse.tile as tile
 from concourse.masks import make_identity
 
 F32 = mybir.dt.float32
@@ -11,20 +9,20 @@ U32 = mybir.dt.uint32
 U8 = mybir.dt.uint8
 FP8X4 = mybir.dt.float8_e4m3fn_x4
 ALU = mybir.AluOpType
-ACTF = mybir.ActivationFunctionType
+ACT = mybir.ActivationFunctionType
 
 P = 128
-B, D_FEAT, N_EX, N_LAB = 8192, 1024, 512, 128
+ROWS, FEATURES, EXEMPLARS, LABELS = 8192, 1024, 512, 128
 EPS = 1e-12
-FLOPS = 2 * B * D_FEAT * N_EX + 2 * B * N_EX * N_LAB
+FLOPS = 2 * ROWS * FEATURES * EXEMPLARS + 2 * ROWS * EXEMPLARS * LABELS
 
+PACK = 4
+F_PASSES = FEATURES // (P * PACK)
 CHUNK_TILES = 4
-N_CHUNKS = B // (P * CHUNK_TILES)
-GT = 2
-NG = B // (P * GT)
-PIN = True
-TAIL_G = NG - 1
-TAIL_BANKS = NG - 3
+N_CHUNKS = ROWS // (P * CHUNK_TILES)
+GROUP_TILES = 2
+N_GROUPS = ROWS // (P * GROUP_TILES)
+BORROWERS = 3
 
 
 def tile_minerva_pa_t_kernel(tc, f_norm, e_norm, ex_class_reps, out):
@@ -34,225 +32,269 @@ def tile_minerva_pa_t_kernel(tc, f_norm, e_norm, ex_class_reps, out):
         loads = ctx.enter_context(tc.tile_pool(name="loads", bufs=N_CHUNKS))
         work = ctx.enter_context(tc.tile_pool(name="work", bufs=2))
         psum = ctx.enter_context(tc.psum_pool(name="psum", bufs=1))
-        if PIN:
-            ctx.enter_context(tc.manual_schedule())
+        ctx.enter_context(tc.manual_schedule())
 
-        ident_f = const.tile([P, P], F32)
-        make_identity(nc, ident_f[:])
-        ident_b = const.tile([P, P], BF16)
-        make_identity(nc, ident_b[:])
+        identity_f32 = const.tile([P, P], F32)
+        make_identity(nc, identity_f32[:])
+        identity_bf16 = const.tile([P, P], BF16)
+        make_identity(nc, identity_bf16[:])
 
-        es = const.tile([P, 4 * D_FEAT], BF16)
-        e_rows = e_norm.rearrange("(p j) k -> p j k", j=4)
-        fs = []
+        f_chunks = []
         for c in range(N_CHUNKS):
-            fs_c = loads.tile([P, CHUNK_TILES * D_FEAT], BF16, tag="fs", name="fs_c")
-            fs.append(fs_c)
-        rs = const.tile([P, 4, N_LAB], BF16)
+            f_chunk = loads.tile([P, CHUNK_TILES * FEATURES], BF16, tag="f_chunk")
+            f_chunks.append(f_chunk)
+        e_rows = const.tile([P, PACK * FEATURES], BF16)
+        r_rows = const.tile([P, PACK, LABELS], BF16)
 
-        def load_f(c, lo, hi):
-            rows = f_norm[c * P * CHUNK_TILES : (c + 1) * P * CHUNK_TILES, :]
+        def load_f(c, first_tile, end_tile):
+            rows = f_norm[c * P * CHUNK_TILES : (c + 1) * P * CHUNK_TILES, :].rearrange("(p t) k -> p t k", t=CHUNK_TILES)
             nc.sync.dma_start(
-                out=fs[c][:, lo * D_FEAT : hi * D_FEAT],
-                in_=rows.rearrange("(p t) k -> p t k", t=CHUNK_TILES)[:, lo:hi, :].rearrange("p t k -> p (t k)"),
+                out=f_chunks[c][:, first_tile * FEATURES : end_tile * FEATURES],
+                in_=rows[:, first_tile:end_tile, :].rearrange("p t k -> p (t k)"),
             )
 
-        load_f(0, 0, GT)
-        for j in range(4):
-            nc.sync.dma_start(out=es[:, j * D_FEAT : (j + 1) * D_FEAT], in_=e_rows[:, j, :])
-        load_f(0, GT, CHUNK_TILES)
-        nc.sync.dma_start(out=rs[:], in_=ex_class_reps.rearrange("(q t) l -> q t l", t=4))
+        load_f(0, 0, GROUP_TILES)
+        for j in range(PACK):
+            nc.sync.dma_start(
+                out=e_rows[:, j * FEATURES : (j + 1) * FEATURES],
+                in_=e_norm.rearrange("(p j) k -> p j k", j=PACK)[:, j, :],
+            )
+        load_f(0, GROUP_TILES, CHUNK_TILES)
+        nc.sync.dma_start(out=r_rows[:], in_=ex_class_reps.rearrange("(q t) l -> q t l", t=PACK))
         for c in range(1, N_CHUNKS):
             load_f(c, 0, CHUNK_TILES)
 
-        def word_transposes(dst, words):
-            for g in range(2):
+        def transpose_pairs(bank, pairs):
+            for h in range(F_PASSES):
                 for u in range(2):
-                    lo = 256 * g + 128 * u
-                    nc.tensor.transpose(dst[:, g, u, :], words[:, lo : lo + P], ident_f[:])
+                    first = (2 * h + u) * P
+                    nc.tensor.transpose(bank[:, h, u, :], pairs[:, first : first + P], identity_f32[:])
 
-        eg = const.tile([P, 4 * 2 * N_EX], BF16, align_bytes=64)
-        egw = eg[:].bitcast(F32).rearrange("p (g j b u) -> p g j b u", g=2, j=4, b=P, u=2)
-        ec = const.tile([P, 2 * N_EX], U32, align_bytes=64)
-        esc = const.tile([P, 2 * N_EX], U8, align_bytes=64)
-        esw = es[:].bitcast(F32)
+        def pairs_side_by_side(bank):
+            return bank[:].rearrange("q h u r -> q h r u")
 
-        def e_transpose():
-            for j in range(4):
-                et = psum.tile([P, 2, 2, P], F32, tag="s", bufs=4, name="et")
-                word_transposes(et, esw[:, 512 * j : 512 * (j + 1)])
-                src = et[:].rearrange("p g u b -> p g b u")
+        e_grouped = const.tile([P, F_PASSES * EXEMPLARS * PACK], BF16, align_bytes=64)
+        e_codes = const.tile([P, F_PASSES * EXEMPLARS], U32, align_bytes=64)
+        e_scales = const.tile([P, F_PASSES * EXEMPLARS], U8, align_bytes=64)
+
+        def transpose_e():
+            e_pairs = e_rows[:].bitcast(F32)
+            grouped = e_grouped[:].bitcast(F32).rearrange("q (h j r u) -> q h j r u", h=F_PASSES, j=PACK, r=P, u=2)
+            for j in range(PACK):
+                bank = psum.tile([P, F_PASSES, 2, P], F32, tag="s_bank", bufs=2 * GROUP_TILES, name="e_bank")
+                transpose_pairs(bank, e_pairs[:, j * FEATURES // 2 : (j + 1) * FEATURES // 2])
                 if j % 2 == 0:
-                    nc.scalar.copy(out=egw[:, :, j, :, :], in_=src)
+                    nc.scalar.copy(out=grouped[:, :, j, :, :], in_=pairs_side_by_side(bank))
                 else:
-                    nc.vector.tensor_copy(out=egw[:, :, j, :, :], in_=src)
+                    nc.vector.tensor_copy(out=grouped[:, :, j, :, :], in_=pairs_side_by_side(bank))
 
-        def e_quantise():
-            for g in range(2):
+        def quantise_e():
+            for h in range(F_PASSES):
                 nc.vector.quantize_mx(
-                    out=ec[:, g * N_EX : (g + 1) * N_EX].bitcast(FP8X4),
-                    scales=esc[:, g * N_EX : (g + 1) * N_EX],
-                    in_=eg[:, g * 4 * N_EX : (g + 1) * 4 * N_EX],
+                    out=e_codes[:, h * EXEMPLARS : (h + 1) * EXEMPLARS].bitcast(FP8X4),
+                    scales=e_scales[:, h * EXEMPLARS : (h + 1) * EXEMPLARS],
+                    in_=e_grouped[:, h * EXEMPLARS * PACK : (h + 1) * EXEMPLARS * PACK],
                 )
 
-        rg = const.tile([P, N_LAB, 4], BF16, align_bytes=64)
-        rc = const.tile([P, N_LAB], U32, align_bytes=64)
-        rsc = const.tile([P, N_LAB], U8, align_bytes=64)
+        r_grouped = const.tile([P, LABELS, PACK], BF16, align_bytes=64)
+        r_codes = const.tile([P, LABELS], U32, align_bytes=64)
+        r_scales = const.tile([P, LABELS], U8, align_bytes=64)
 
-        def r_prep():
-            nc.vector.tensor_copy(out=rg[:], in_=rs[:].rearrange("q t l -> q l t"))
-            nc.vector.quantize_mx(out=rc[:].bitcast(FP8X4), scales=rsc[:], in_=rg[:].rearrange("q l t -> q (l t)"))
+        def quantise_r():
+            nc.vector.tensor_copy(out=r_grouped[:], in_=r_rows[:].rearrange("q t l -> q l t"))
+            nc.vector.quantize_mx(
+                out=r_codes[:].bitcast(FP8X4), scales=r_scales[:], in_=r_grouped[:].rearrange("q l t -> q (l t)")
+            )
 
-        st = {}
+        alive = {}
 
-        def ok(g):
-            return 0 <= g < NG
+        def absent(g):
+            return g < 0 or g >= N_GROUPS
 
-        def t_f(g):
-            for j in range(GT):
-                t = g * GT + j
-                ft = psum.tile([P, 2, 2, P], F32, tag="ft", bufs=2, name="ft")
-                words = fs[t // CHUNK_TILES][:].bitcast(F32)
-                lo = 512 * (t % CHUNK_TILES)
-                word_transposes(ft, words[:, lo : lo + 512])
-                st[("ft", g, j)] = ft
+        def transpose_f(g):
+            if absent(g):
+                return
+            for j in range(GROUP_TILES):
+                t = g * GROUP_TILES + j
+                pairs = f_chunks[t // CHUNK_TILES][:].bitcast(F32)
+                first = (t % CHUNK_TILES) * FEATURES // 2
+                bank = psum.tile([P, F_PASSES, 2, P], F32, tag="f_bank", bufs=GROUP_TILES, name="f_bank")
+                transpose_pairs(bank, pairs[:, first : first + FEATURES // 2])
+                alive[("f_bank", g, j)] = bank
 
-        def op_a(g):
-            fg = work.tile([P, GT * 2 * P * 4], BF16, tag="fg", bufs=3, align_bytes=64, name="fg")
-            fgw = fg[:].bitcast(F32).rearrange("p (j g b u) -> p j g b u", j=GT, g=2, b=P, u=2)
-            for j in range(GT):
-                nc.scalar.copy(out=fgw[:, j], in_=st[("ft", g, j)][:].rearrange("p g u b -> p g b u"))
-            st[("fg", g)] = fg
+        def regroup_f(g):
+            if absent(g):
+                return
+            f_grouped = work.tile([P, GROUP_TILES * FEATURES], BF16, tag="f_grouped", align_bytes=64)
+            grouped = f_grouped[:].bitcast(F32).rearrange("q (j h r u) -> q j h r u", j=GROUP_TILES, h=F_PASSES, r=P, u=2)
+            for j in range(GROUP_TILES):
+                nc.scalar.copy(out=grouped[:, j], in_=pairs_side_by_side(alive[("f_bank", g, j)]))
+            alive[("f_grouped", g)] = f_grouped
 
-        def op_b(g):
-            fc = work.tile([P, GT * 2 * P], U32, tag="fc", bufs=3, align_bytes=64, name="fc")
-            fsc = work.tile([P, GT * 2 * P], U8, tag="fsc", bufs=3, align_bytes=64, name="fsc")
-            nc.vector.quantize_mx(out=fc[:].bitcast(FP8X4), scales=fsc[:], in_=st[("fg", g)][:])
-            st[("fc", g)] = (fc, fsc)
+        def quantise_f(g):
+            if absent(g):
+                return
+            f_codes = work.tile([P, GROUP_TILES * F_PASSES * P], U32, tag="f_codes", bufs=3, align_bytes=64)
+            f_scales = work.tile([P, GROUP_TILES * F_PASSES * P], U8, tag="f_scales", bufs=3, align_bytes=64)
+            nc.vector.quantize_mx(out=f_codes[:].bitcast(FP8X4), scales=f_scales[:], in_=alive[("f_grouped", g)][:])
+            alive[("f_codes", g)] = (f_codes, f_scales)
 
-        def mm1(g):
-            fc, fsc = st[("fc", g)]
-            for j in range(GT):
-                s = psum.tile([P, N_EX], F32, tag="s", bufs=4, name="s")
-                for h in range(2):
-                    lo = (j * 2 + h) * P
+        def similarities(g):
+            if absent(g):
+                return
+            f_codes, f_scales = alive[("f_codes", g)]
+            for j in range(GROUP_TILES):
+                s = psum.tile([P, EXEMPLARS], F32, tag="s_bank", bufs=2 * GROUP_TILES, name="s")
+                for h in range(F_PASSES):
+                    rows = slice((j * F_PASSES + h) * P, (j * F_PASSES + h + 1) * P)
+                    exemplars = slice(h * EXEMPLARS, (h + 1) * EXEMPLARS)
                     nc.tensor.matmul_mx(
                         out=s[:],
-                        lhsT=fc[:, lo : lo + P].bitcast(FP8X4),
-                        lhsT_scale=fsc[:, lo : lo + P],
-                        rhs=ec[:, h * N_EX : (h + 1) * N_EX].bitcast(FP8X4),
-                        rhs_scale=esc[:, h * N_EX : (h + 1) * N_EX],
+                        lhsT=f_codes[:, rows].bitcast(FP8X4),
+                        lhsT_scale=f_scales[:, rows],
+                        rhs=e_codes[:, exemplars].bitcast(FP8X4),
+                        rhs_scale=e_scales[:, exemplars],
                         start=(h == 0),
-                        stop=(h == 1),
+                        stop=(h == F_PASSES - 1),
                     )
-                st[("s", g, j)] = s
+                alive[("s", g, j)] = s
 
-        def op_c(g):
-            for j in range(GT):
-                s2 = work.tile([P, N_EX], F32, tag="s2", bufs=4, name="s2")
-                nc.scalar.activation(out=s2[:], in_=st[("s", g, j)][:], func=ACTF.Square)
-                st[("s2", g, j)] = s2
+        def square(g):
+            if absent(g):
+                return
+            for j in range(GROUP_TILES):
+                s_squared = work.tile([P, EXEMPLARS], F32, tag="s_squared", bufs=2 * GROUP_TILES)
+                nc.scalar.activation(out=s_squared[:], in_=alive[("s", g, j)][:], func=ACT.Square)
+                alive[("s_squared", g, j)] = s_squared
 
-        def op_d(g):
-            for j in range(GT):
-                a = work.tile([P, N_EX], F32, tag="a", bufs=8, name="a")
-                nc.vector.tensor_tensor(out=a[:], in0=st[("s", g, j)][:], in1=st[("s2", g, j)][:], op=ALU.mult)
-                st[("a", g, j)] = a
+        def cube(g):
+            if absent(g):
+                return
+            for j in range(GROUP_TILES):
+                a = work.tile([P, EXEMPLARS], F32, tag="a", bufs=3 * GROUP_TILES)
+                nc.vector.tensor_tensor(out=a[:], in0=alive[("s", g, j)][:], in1=alive[("s_squared", g, j)][:], op=ALU.mult)
+                alive[("a", g, j)] = a
 
-        def op_e(g):
-            sums = work.tile([P, GT], F32, tag="sums", bufs=4, name="sums")
-            for j in range(GT):
-                junk = work.tile([P, N_EX], BF16, tag="junk", bufs=2, name="junk")
-                nc.scalar.activation(out=junk[:], in_=st[("a", g, j)][:], func=ACTF.Abs, accum_out=sums[:, j : j + 1])
-            st[("sums", g)] = sums
+        def row_sums(g):
+            if absent(g):
+                return
+            sums = work.tile([P, GROUP_TILES], F32, tag="sums")
+            for j in range(GROUP_TILES):
+                magnitudes = work.tile([P, EXEMPLARS], BF16, tag="magnitudes")
+                nc.scalar.activation(
+                    out=magnitudes[:], in_=alive[("a", g, j)][:], func=ACT.Abs, accum_out=sums[:, j : j + 1]
+                )
+            alive[("sums", g)] = sums
 
-        def op_f1(g):
-            floor = work.tile([P, GT], F32, tag="floor", bufs=2, name="floor")
-            nc.vector.tensor_scalar_max(out=floor[:], in0=st[("sums", g)][:], scalar1=EPS)
-            st[("floor", g)] = floor
+        def floor_sums(g):
+            if absent(g):
+                return
+            floored = work.tile([P, GROUP_TILES], F32, tag="floored")
+            nc.vector.tensor_scalar_max(out=floored[:], in0=alive[("sums", g)][:], scalar1=EPS)
+            alive[("floored", g)] = floored
 
-        def op_f2(g):
-            rin = work.tile([P, GT], F32, tag="rin", bufs=3, name="rin")
-            nc.vector.reciprocal(out=rin[:], in_=st[("floor", g)][:])
-            st[("rin", g)] = rin
+        def invert_sums(g):
+            if absent(g):
+                return
+            inverse = work.tile([P, GROUP_TILES], F32, tag="inverse")
+            nc.vector.reciprocal(out=inverse[:], in_=alive[("floored", g)][:])
+            alive[("inverse", g)] = inverse
 
-        def op_g(g):
-            rin = st[("rin", g)]
-            p = work.tile([P, GT, N_EX], BF16, tag="p", bufs=3, name="p")
-            for j in range(GT):
-                if g < TAIL_G:
-                    nc.gpsimd.tensor_scalar(
-                        out=p[:, j, :], in0=st[("a", g, j)][:], scalar1=rin[:, j : j + 1], scalar2=0.0,
-                        op0=ALU.mult, op1=ALU.add,
-                    )
-                else:
-                    nc.vector.tensor_scalar(
-                        out=p[:, j, :], in0=st[("a", g, j)][:], scalar1=rin[:, j : j + 1], scalar2=None, op0=ALU.mult
-                    )
-            st[("p", g)] = p
+        def normalise(g):
+            if absent(g):
+                return
+            inverse = alive[("inverse", g)]
+            p = work.tile([P, GROUP_TILES, EXEMPLARS], BF16, tag="p", bufs=3)
+            for j in range(GROUP_TILES):
+                nc.gpsimd.tensor_scalar(
+                    out=p[:, j, :], in0=alive[("a", g, j)][:], scalar1=inverse[:, j : j + 1], scalar2=0.0,
+                    op0=ALU.mult, op1=ALU.add,
+                )
+            alive[("p", g)] = p
 
-        def t_p(g):
-            p = st[("p", g)]
-            if g < TAIL_BANKS:
-                pt = psum.tile([P, GT, 4, P], BF16, tag="pt", bufs=1, name="pt")
+        def transpose_p(g):
+            if absent(g):
+                return
+            if g < N_GROUPS - BORROWERS:
+                bank = psum.tile([P, GROUP_TILES, PACK, P], BF16, tag="p_bank", bufs=1, name="p_bank")
             else:
-                pt = psum.tile([P, GT, 4, P], BF16, tag="s", bufs=4, name="pt")
-            for j in range(GT):
-                for t in range(4):
-                    nc.tensor.transpose(pt[:, j, t, :], p[:, j, t * P : (t + 1) * P], ident_b[:])
-            st[("pt", g)] = pt
+                bank = psum.tile([P, GROUP_TILES, PACK, P], BF16, tag="s_bank", bufs=2 * GROUP_TILES, name="p_bank")
+            p = alive[("p", g)]
+            for j in range(GROUP_TILES):
+                for t in range(PACK):
+                    nc.tensor.transpose(bank[:, j, t, :], p[:, j, t * P : (t + 1) * P], identity_bf16[:])
+            alive[("p_bank", g)] = bank
 
-        def op_h(g):
-            pg = work.tile([P, GT, P, 4], BF16, tag="pg", bufs=2, align_bytes=64, name="pg")
-            nc.vector.tensor_copy(out=pg[:], in_=st[("pt", g)][:].rearrange("p j t b -> p j b t"))
-            st[("pg", g)] = pg
+        def regroup_p(g):
+            if absent(g):
+                return
+            p_grouped = work.tile([P, GROUP_TILES, P, PACK], BF16, tag="p_grouped", align_bytes=64)
+            nc.vector.tensor_copy(out=p_grouped[:], in_=alive[("p_bank", g)][:].rearrange("q j t r -> q j r t"))
+            alive[("p_grouped", g)] = p_grouped
 
-        def op_i(g):
-            pc = work.tile([P, GT * P], U32, tag="pc", bufs=2, align_bytes=64, name="pc")
-            psc = work.tile([P, GT * P], U8, tag="psc", bufs=2, align_bytes=64, name="psc")
+        def quantise_p(g):
+            if absent(g):
+                return
+            p_codes = work.tile([P, GROUP_TILES * P], U32, tag="p_codes", align_bytes=64)
+            p_scales = work.tile([P, GROUP_TILES * P], U8, tag="p_scales", align_bytes=64)
             nc.vector.quantize_mx(
-                out=pc[:].bitcast(FP8X4), scales=psc[:], in_=st[("pg", g)][:].rearrange("p j b t -> p (j b t)")
+                out=p_codes[:].bitcast(FP8X4),
+                scales=p_scales[:],
+                in_=alive[("p_grouped", g)][:].rearrange("q j r t -> q (j r t)"),
             )
-            st[("pc", g)] = (pc, psc)
+            alive[("p_codes", g)] = (p_codes, p_scales)
 
-        def mm2(g):
-            pc, psc = st[("pc", g)]
-            if g < TAIL_BANKS:
-                o = psum.tile([P, GT, N_LAB], F32, tag="o", bufs=1, name="o")
+        def read_out(g):
+            if absent(g):
+                return
+            p_codes, p_scales = alive[("p_codes", g)]
+            if g < N_GROUPS - BORROWERS:
+                echo = psum.tile([P, GROUP_TILES, LABELS], F32, tag="echo_bank", bufs=1, name="echo")
             else:
-                o = psum.tile([P, GT, N_LAB], F32, tag="ft", bufs=2, name="o")
-            for j in range(GT):
+                echo = psum.tile([P, GROUP_TILES, LABELS], F32, tag="f_bank", bufs=GROUP_TILES, name="echo")
+            for j in range(GROUP_TILES):
                 nc.tensor.matmul_mx(
-                    out=o[:, j, :],
-                    lhsT=pc[:, j * P : (j + 1) * P].bitcast(FP8X4),
-                    lhsT_scale=psc[:, j * P : (j + 1) * P],
-                    rhs=rc[:].bitcast(FP8X4),
-                    rhs_scale=rsc[:],
+                    out=echo[:, j, :],
+                    lhsT=p_codes[:, j * P : (j + 1) * P].bitcast(FP8X4),
+                    lhsT_scale=p_scales[:, j * P : (j + 1) * P],
+                    rhs=r_codes[:].bitcast(FP8X4),
+                    rhs_scale=r_scales[:],
                     start=True,
                     stop=True,
                 )
-            st[("o", g)] = o
+            alive[("echo", g)] = echo
 
-        def op_j(g):
-            osb = work.tile([P, GT, N_LAB], F32, tag="osb", bufs=3, name="osb")
-            nc.vector.tensor_copy(out=osb[:], in_=st[("o", g)][:])
-            c = (g * GT) // CHUNK_TILES
-            t0 = (g * GT) % CHUNK_TILES
+        def store(g):
+            if absent(g):
+                return
+            echo_rows = work.tile([P, GROUP_TILES, LABELS], F32, tag="echo_rows", bufs=3)
+            nc.vector.tensor_copy(out=echo_rows[:], in_=alive[("echo", g)][:])
+            c = g * GROUP_TILES // CHUNK_TILES
+            first_tile = g * GROUP_TILES % CHUNK_TILES
             rows = out[c * P * CHUNK_TILES : (c + 1) * P * CHUNK_TILES, :].rearrange("(p t) l -> p t l", t=CHUNK_TILES)
-            nc.sync.dma_start(out=rows[:, t0 : t0 + GT, :], in_=osb[:])
+            nc.sync.dma_start(out=rows[:, first_tile : first_tile + GROUP_TILES, :], in_=echo_rows[:])
 
-        plan = (
-            (op_i, -5), (t_p, -4), (op_a, 2), (mm1, 0), (op_j, -6), (op_d, -1), (op_h, -4), (op_c, 0),
-            (mm2, -5), (op_f1, -2), (t_f, 3), (op_e, -1), (op_b, 2), (op_f2, -2), (op_g, -2),
-        )
-        t_f(0)
-        op_a(0)
-        e_transpose()
-        op_b(0)
-        e_quantise()
-        r_prep()
-        early = ((t_f, 0), (op_a, 0), (op_b, 0))
-        for i in range(-3, NG + 6):
-            for fn, d in plan:
-                if ok(i + d) and (fn, i + d) not in early:
-                    fn(i + d)
+        transpose_f(0)
+        regroup_f(0)
+        transpose_e()
+        quantise_f(0)
+        quantise_e()
+        quantise_r()
+        transpose_f(1)
+
+        for period in range(-1, N_GROUPS + 6):
+            quantise_p(period - 5)
+            transpose_p(period - 4)
+            regroup_f(period + 2)
+            similarities(period)
+            store(period - 6)
+            cube(period - 1)
+            regroup_p(period - 4)
+            square(period)
+            read_out(period - 5)
+            floor_sums(period - 2)
+            transpose_f(period + 3)
+            row_sums(period - 1)
+            quantise_f(period + 2)
+            invert_sums(period - 2)
+            normalise(period - 2)

@@ -36,15 +36,13 @@ def tile_minerva_pa_t_kernel(tc, f_norm, e_norm, ex_class_reps, out):
 
         identity_f32 = const.tile([P, P], F32)
         make_identity(nc, identity_f32[:])
-        identity_bf16 = const.tile([P, P], BF16)
-        make_identity(nc, identity_bf16[:])
 
         f_chunks = []
         for c in range(N_CHUNKS):
             f_chunk = loads.tile([P, CHUNK_TILES * FEATURES], BF16, tag="f_chunk")
             f_chunks.append(f_chunk)
         e_rows = const.tile([P, PACK * FEATURES], BF16)
-        r_rows = const.tile([P, PACK, LABELS], BF16)
+        r_rows = const.tile([P, 2, 2, LABELS], BF16)
 
         def load_f(c, first_tile, end_tile):
             rows = f_norm[c * P * CHUNK_TILES : (c + 1) * P * CHUNK_TILES, :].rearrange("(p t) k -> p t k", t=CHUNK_TILES)
@@ -57,10 +55,10 @@ def tile_minerva_pa_t_kernel(tc, f_norm, e_norm, ex_class_reps, out):
         for j in range(PACK):
             nc.sync.dma_start(
                 out=e_rows[:, j * FEATURES : (j + 1) * FEATURES],
-                in_=e_norm.rearrange("(p j) k -> p j k", j=PACK)[:, j, :],
+                in_=e_norm[j * P : (j + 1) * P, :],
             )
         load_f(0, GROUP_TILES, CHUNK_TILES)
-        nc.sync.dma_start(out=r_rows[:], in_=ex_class_reps.rearrange("(q t) l -> q t l", t=PACK))
+        nc.sync.dma_start(out=r_rows[:], in_=ex_class_reps.rearrange("(u q e) l -> q u e l", u=2, e=2))
         for c in range(1, N_CHUNKS):
             load_f(c, 0, CHUNK_TILES)
 
@@ -101,7 +99,7 @@ def tile_minerva_pa_t_kernel(tc, f_norm, e_norm, ex_class_reps, out):
         r_scales = const.tile([P, LABELS], U8, align_bytes=64)
 
         def quantise_r():
-            nc.vector.tensor_copy(out=r_grouped[:], in_=r_rows[:].rearrange("q t l -> q l t"))
+            nc.vector.tensor_copy(out=r_grouped[:], in_=r_rows[:].rearrange("q u e l -> q l (u e)"))
             nc.vector.quantize_mx(
                 out=r_codes[:].bitcast(FP8X4), scales=r_scales[:], in_=r_grouped[:].rearrange("q l t -> q (l t)")
             )
@@ -216,20 +214,22 @@ def tile_minerva_pa_t_kernel(tc, f_norm, e_norm, ex_class_reps, out):
             if absent(g):
                 return
             if g < N_GROUPS - BORROWERS:
-                bank = psum.tile([P, GROUP_TILES, PACK, P], BF16, tag="p_bank", bufs=1, name="p_bank")
+                bank = psum.tile([P, GROUP_TILES, 2, P], F32, tag="p_bank", bufs=1, name="p_bank")
             else:
-                bank = psum.tile([P, GROUP_TILES, PACK, P], BF16, tag="s_bank", bufs=2 * GROUP_TILES, name="p_bank")
-            p = alive[("p", g)]
+                bank = psum.tile([P, GROUP_TILES, 2, P], F32, tag="s_bank", bufs=2 * GROUP_TILES, name="p_bank")
+            words = alive[("p", g)][:].rearrange("r j c -> r (j c)").bitcast(F32)
             for j in range(GROUP_TILES):
-                for t in range(PACK):
-                    nc.tensor.transpose(bank[:, j, t, :], p[:, j, t * P : (t + 1) * P], identity_bf16[:])
+                for u in range(2):
+                    first = (2 * j + u) * P
+                    nc.tensor.transpose(bank[:, j, u, :], words[:, first : first + P], identity_f32[:])
             alive[("p_bank", g)] = bank
 
         def regroup_p(g):
             if absent(g):
                 return
-            p_grouped = work.tile([P, GROUP_TILES, P, PACK], BF16, tag="p_grouped", align_bytes=64)
-            nc.vector.tensor_copy(out=p_grouped[:], in_=alive[("p_bank", g)][:].rearrange("q j t r -> q j r t"))
+            p_grouped = work.tile([P, GROUP_TILES * EXEMPLARS], BF16, tag="p_grouped", align_bytes=64)
+            grouped = p_grouped[:].bitcast(F32).rearrange("q (j r u) -> q j r u", j=GROUP_TILES, r=P, u=2)
+            nc.vector.tensor_copy(out=grouped, in_=alive[("p_bank", g)][:].rearrange("q j u r -> q j r u"))
             alive[("p_grouped", g)] = p_grouped
 
         def quantise_p(g):
@@ -240,7 +240,7 @@ def tile_minerva_pa_t_kernel(tc, f_norm, e_norm, ex_class_reps, out):
             nc.vector.quantize_mx(
                 out=p_codes[:].bitcast(FP8X4),
                 scales=p_scales[:],
-                in_=alive[("p_grouped", g)][:].rearrange("q j r t -> q (j r t)"),
+                in_=alive[("p_grouped", g)][:],
             )
             alive[("p_codes", g)] = (p_codes, p_scales)
 

@@ -10,6 +10,7 @@ U8 = mybir.dt.uint8
 FP8X4 = mybir.dt.float8_e4m3fn_x4
 ALU = mybir.AluOpType
 ACT = mybir.ActivationFunctionType
+AXES = mybir.AxisListType
 
 P = 128
 ROWS, FEATURES, EXEMPLARS, LABELS = 8192, 1024, 512, 128
@@ -23,6 +24,7 @@ N_CHUNKS = ROWS // (P * CHUNK_TILES)
 GROUP_TILES = 2
 N_GROUPS = ROWS // (P * GROUP_TILES)
 BORROWERS = 3
+VECTOR_SUMS = 3
 
 
 def tile_minerva_pa_t_kernel(tc, f_norm, e_norm, ex_class_reps, out):
@@ -178,6 +180,11 @@ def tile_minerva_pa_t_kernel(tc, f_norm, e_norm, ex_class_reps, out):
                 return
             sums = work.tile([P, GROUP_TILES], F32, tag="sums")
             for j in range(GROUP_TILES):
+                if j == 1 and g % VECTOR_SUMS == 0:
+                    nc.vector.tensor_reduce(
+                        out=sums[:, j : j + 1], in_=alive[("a", g, j)][:], axis=AXES.X, op=ALU.add, apply_absolute_value=True
+                    )
+                    continue
                 magnitudes = work.tile([P, EXEMPLARS], BF16, tag="magnitudes")
                 nc.scalar.activation(
                     out=magnitudes[:], in_=alive[("a", g, j)][:], func=ACT.Abs, accum_out=sums[:, j : j + 1]

@@ -24,7 +24,7 @@ N_CHUNKS = ROWS // (P * CHUNK_TILES)
 GROUP_TILES = 2
 N_GROUPS = ROWS // (P * GROUP_TILES)
 BORROWERS = 3
-VECTOR_SUMS = 3
+SCALAR_SUMS = 5
 
 
 def tile_minerva_pa_t_kernel(tc, f_norm, e_norm, ex_class_reps, out):
@@ -53,15 +53,19 @@ def tile_minerva_pa_t_kernel(tc, f_norm, e_norm, ex_class_reps, out):
                 in_=rows[:, first_tile:end_tile, :].rearrange("p t k -> p (t k)"),
             )
 
-        load_f(0, 0, GROUP_TILES)
+        for t in range(GROUP_TILES):
+            load_f(0, t, t + 1)
         for j in range(PACK):
             nc.sync.dma_start(
                 out=e_rows[:, j * FEATURES : (j + 1) * FEATURES],
                 in_=e_norm[j * P : (j + 1) * P, :],
             )
-        load_f(0, GROUP_TILES, CHUNK_TILES)
+        for t in range(GROUP_TILES, CHUNK_TILES):
+            load_f(0, t, t + 1)
         nc.sync.dma_start(out=r_rows[:], in_=ex_class_reps.rearrange("(u q e) l -> q u e l", u=2, e=2))
-        for c in range(1, N_CHUNKS):
+        load_f(1, 0, GROUP_TILES)
+        load_f(1, GROUP_TILES, CHUNK_TILES)
+        for c in range(2, N_CHUNKS):
             load_f(c, 0, CHUNK_TILES)
 
         def transpose_pairs(bank, pairs):
@@ -128,7 +132,11 @@ def tile_minerva_pa_t_kernel(tc, f_norm, e_norm, ex_class_reps, out):
             f_grouped = work.tile([P, GROUP_TILES * FEATURES], BF16, tag="f_grouped", align_bytes=64)
             grouped = f_grouped[:].bitcast(F32).rearrange("q (j h r u) -> q j h r u", j=GROUP_TILES, h=F_PASSES, r=P, u=2)
             for j in range(GROUP_TILES):
-                nc.scalar.copy(out=grouped[:, j], in_=pairs_side_by_side(alive[("f_bank", g, j)]))
+                words = pairs_side_by_side(alive[("f_bank", g, j)])
+                if g == 0 and j == 1:
+                    nc.vector.tensor_copy(out=grouped[:, j], in_=words)
+                else:
+                    nc.scalar.copy(out=grouped[:, j], in_=words)
             alive[("f_grouped", g)] = f_grouped
 
         def quantise_f(g):
@@ -180,22 +188,22 @@ def tile_minerva_pa_t_kernel(tc, f_norm, e_norm, ex_class_reps, out):
                 return
             sums = work.tile([P, GROUP_TILES], F32, tag="sums")
             for j in range(GROUP_TILES):
-                if j == 1 and g % VECTOR_SUMS == 0:
+                if j == 1 and g % SCALAR_SUMS == 1:
+                    magnitudes = work.tile([P, EXEMPLARS], BF16, tag="magnitudes")
+                    nc.scalar.activation(
+                        out=magnitudes[:], in_=alive[("a", g, j)][:], func=ACT.Abs, accum_out=sums[:, j : j + 1]
+                    )
+                else:
                     nc.vector.tensor_reduce(
                         out=sums[:, j : j + 1], in_=alive[("a", g, j)][:], axis=AXES.X, op=ALU.add, apply_absolute_value=True
                     )
-                    continue
-                magnitudes = work.tile([P, EXEMPLARS], BF16, tag="magnitudes")
-                nc.scalar.activation(
-                    out=magnitudes[:], in_=alive[("a", g, j)][:], func=ACT.Abs, accum_out=sums[:, j : j + 1]
-                )
             alive[("sums", g)] = sums
 
         def floor_sums(g):
             if absent(g):
                 return
             floored = work.tile([P, GROUP_TILES], F32, tag="floored")
-            nc.vector.tensor_scalar_max(out=floored[:], in0=alive[("sums", g)][:], scalar1=EPS)
+            nc.gpsimd.tensor_scalar_max(out=floored[:], in0=alive[("sums", g)][:], scalar1=EPS)
             alive[("floored", g)] = floored
 
         def invert_sums(g):
@@ -236,7 +244,7 @@ def tile_minerva_pa_t_kernel(tc, f_norm, e_norm, ex_class_reps, out):
                 return
             p_grouped = work.tile([P, GROUP_TILES * EXEMPLARS], BF16, tag="p_grouped", align_bytes=64)
             grouped = p_grouped[:].bitcast(F32).rearrange("q (j r u) -> q j r u", j=GROUP_TILES, r=P, u=2)
-            nc.vector.tensor_copy(out=grouped, in_=alive[("p_bank", g)][:].rearrange("q j u r -> q j r u"))
+            nc.scalar.copy(out=grouped, in_=alive[("p_bank", g)][:].rearrange("q j u r -> q j r u"))
             alive[("p_grouped", g)] = p_grouped
 
         def quantise_p(g):
@@ -274,8 +282,8 @@ def tile_minerva_pa_t_kernel(tc, f_norm, e_norm, ex_class_reps, out):
         def store(g):
             if absent(g):
                 return
-            echo_rows = work.tile([P, GROUP_TILES, LABELS], F32, tag="echo_rows", bufs=3)
-            nc.vector.tensor_copy(out=echo_rows[:], in_=alive[("echo", g)][:])
+            echo_rows = work.tile([P, GROUP_TILES, LABELS], F32, tag="echo_rows", bufs=8)
+            nc.scalar.copy(out=echo_rows[:], in_=alive[("echo", g)][:])
             c = g * GROUP_TILES // CHUNK_TILES
             first_tile = g * GROUP_TILES % CHUNK_TILES
             rows = out[c * P * CHUNK_TILES : (c + 1) * P * CHUNK_TILES, :].rearrange("(p t) l -> p t l", t=CHUNK_TILES)
@@ -289,19 +297,19 @@ def tile_minerva_pa_t_kernel(tc, f_norm, e_norm, ex_class_reps, out):
         quantise_r()
         transpose_f(1)
 
-        for period in range(-1, N_GROUPS + 6):
-            quantise_p(period - 5)
-            transpose_p(period - 4)
+        for period in range(-1, N_GROUPS + 5):
+            quantise_p(period - 4)
+            transpose_p(period - 3)
             regroup_f(period + 2)
             similarities(period)
-            store(period - 6)
-            cube(period - 1)
-            regroup_p(period - 4)
-            square(period)
-            read_out(period - 5)
-            floor_sums(period - 2)
-            transpose_f(period + 3)
-            row_sums(period - 1)
-            quantise_f(period + 2)
             invert_sums(period - 2)
             normalise(period - 2)
+            cube(period - 1)
+            store(period - 5)
+            regroup_p(period - 3)
+            square(period)
+            read_out(period - 4)
+            row_sums(period - 1)
+            transpose_f(period + 3)
+            quantise_f(period + 2)
+            floor_sums(period - 1)

@@ -203,7 +203,7 @@ def tile_minerva_pa_t_kernel(tc, f_norm, e_norm, ex_class_reps, out):
             if absent(g):
                 return
             floored = work.tile([P, GROUP_TILES], F32, tag="floored")
-            nc.gpsimd.tensor_scalar_max(out=floored[:], in0=alive[("sums", g)][:], scalar1=EPS)
+            nc.vector.tensor_scalar_max(out=floored[:], in0=alive[("sums", g)][:], scalar1=EPS)
             alive[("floored", g)] = floored
 
         def invert_sums(g):

@@ -24,7 +24,9 @@ N_CHUNKS = ROWS // (P * CHUNK_TILES)
 GROUP_TILES = 2
 N_GROUPS = ROWS // (P * GROUP_TILES)
 BORROWERS = 3
-SCALAR_SUMS = 5
+SINGLE_FRONT = 2
+SINGLE_BACK = N_GROUPS - 2
+VECTOR_LAST = 3
 
 
 def tile_minerva_pa_t_kernel(tc, f_norm, e_norm, ex_class_reps, out):
@@ -112,204 +114,286 @@ def tile_minerva_pa_t_kernel(tc, f_norm, e_norm, ex_class_reps, out):
 
         alive = {}
 
-        def absent(g):
-            return g < 0 or g >= N_GROUPS
+        def here(groups):
+            return [g for g in groups if 0 <= g < N_GROUPS]
 
-        def transpose_f(g):
-            if absent(g):
-                return
-            for j in range(GROUP_TILES):
+        def front_pair(g):
+            return [g] if g < SINGLE_FRONT else [g - g % 2, g - g % 2 + 1]
+
+        def sums_pair(g):
+            return here([g - 1, g] if g % 2 == 0 else [g, g + 1])
+
+        def back_pair(g):
+            return [g] if g >= SINGLE_BACK else [g - g % 2, g - g % 2 + 1]
+
+        def transpose_f(g, j):
+            for g in here([g]):
                 t = g * GROUP_TILES + j
                 pairs = f_chunks[t // CHUNK_TILES][:].bitcast(F32)
                 first = (t % CHUNK_TILES) * FEATURES // 2
-                bank = psum.tile([P, F_PASSES, 2, P], F32, tag="f_bank", bufs=GROUP_TILES, name="f_bank")
+                bank = psum.tile([P, F_PASSES, 2, P], F32, tag="f_bank", bufs=2, name="f_bank")
                 transpose_pairs(bank, pairs[:, first : first + FEATURES // 2])
                 alive[("f_bank", g, j)] = bank
 
-        def regroup_f(g):
-            if absent(g):
-                return
-            f_grouped = work.tile([P, GROUP_TILES * FEATURES], BF16, tag="f_grouped", align_bytes=64)
-            grouped = f_grouped[:].bitcast(F32).rearrange("q (j h r u) -> q j h r u", j=GROUP_TILES, h=F_PASSES, r=P, u=2)
-            for j in range(GROUP_TILES):
+        def regroup_f(g, j):
+            for g in here([g]):
+                groups = front_pair(g)
+                n = len(groups) * GROUP_TILES
+                if g == groups[0] and j == 0:
+                    f_grouped = work.tile([P, n * FEATURES], BF16, tag="f_grouped", align_bytes=64)
+                    alive[("f_grouped", g)] = f_grouped
+                f_grouped = alive[("f_grouped", groups[0])]
+                grouped = f_grouped[:].bitcast(F32).rearrange("q (i h r u) -> q i h r u", i=n, h=F_PASSES, r=P, u=2)
+                i = groups.index(g) * GROUP_TILES + j
                 words = pairs_side_by_side(alive[("f_bank", g, j)])
                 if g == 0 and j == 1:
-                    nc.vector.tensor_copy(out=grouped[:, j], in_=words)
+                    nc.vector.tensor_copy(out=grouped[:, i], in_=words)
                 else:
-                    nc.scalar.copy(out=grouped[:, j], in_=words)
-            alive[("f_grouped", g)] = f_grouped
+                    nc.scalar.copy(out=grouped[:, i], in_=words)
 
         def quantise_f(g):
-            if absent(g):
-                return
-            f_codes = work.tile([P, GROUP_TILES * F_PASSES * P], U32, tag="f_codes", bufs=3, align_bytes=64)
-            f_scales = work.tile([P, GROUP_TILES * F_PASSES * P], U8, tag="f_scales", bufs=3, align_bytes=64)
-            nc.vector.quantize_mx(out=f_codes[:].bitcast(FP8X4), scales=f_scales[:], in_=alive[("f_grouped", g)][:])
-            alive[("f_codes", g)] = (f_codes, f_scales)
+            for g in here([g]):
+                n = len(front_pair(g)) * GROUP_TILES * F_PASSES * P
+                f_codes = work.tile([P, n], U32, tag="f_codes", bufs=3, align_bytes=64)
+                f_scales = work.tile([P, n], U8, tag="f_scales", bufs=3, align_bytes=64)
+                nc.vector.quantize_mx(out=f_codes[:].bitcast(FP8X4), scales=f_scales[:], in_=alive[("f_grouped", g)][:])
+                alive[("f_codes", g)] = (f_codes, f_scales)
 
         def similarities(g):
-            if absent(g):
-                return
-            f_codes, f_scales = alive[("f_codes", g)]
-            for j in range(GROUP_TILES):
-                s = psum.tile([P, EXEMPLARS], F32, tag="s_bank", bufs=2 * GROUP_TILES, name="s")
-                for h in range(F_PASSES):
-                    rows = slice((j * F_PASSES + h) * P, (j * F_PASSES + h + 1) * P)
-                    exemplars = slice(h * EXEMPLARS, (h + 1) * EXEMPLARS)
-                    nc.tensor.matmul_mx(
-                        out=s[:],
-                        lhsT=f_codes[:, rows].bitcast(FP8X4),
-                        lhsT_scale=f_scales[:, rows],
-                        rhs=e_codes[:, exemplars].bitcast(FP8X4),
-                        rhs_scale=e_scales[:, exemplars],
-                        start=(h == 0),
-                        stop=(h == F_PASSES - 1),
-                    )
-                alive[("s", g, j)] = s
+            for g in here([g]):
+                groups = front_pair(g)
+                f_codes, f_scales = alive[("f_codes", groups[0])]
+                for j in range(GROUP_TILES):
+                    s = psum.tile([P, EXEMPLARS], F32, tag="s_bank", bufs=2 * GROUP_TILES, name="s")
+                    for h in range(F_PASSES):
+                        k = (groups.index(g) * GROUP_TILES + j) * F_PASSES + h
+                        rows = slice(k * P, (k + 1) * P)
+                        exemplars = slice(h * EXEMPLARS, (h + 1) * EXEMPLARS)
+                        nc.tensor.matmul_mx(
+                            out=s[:],
+                            lhsT=f_codes[:, rows].bitcast(FP8X4),
+                            lhsT_scale=f_scales[:, rows],
+                            rhs=e_codes[:, exemplars].bitcast(FP8X4),
+                            rhs_scale=e_scales[:, exemplars],
+                            start=(h == 0),
+                            stop=(h == F_PASSES - 1),
+                        )
+                    alive[("s", g, j)] = s
 
         def square(g):
-            if absent(g):
-                return
-            for j in range(GROUP_TILES):
-                s_squared = work.tile([P, EXEMPLARS], F32, tag="s_squared", bufs=2 * GROUP_TILES)
-                nc.scalar.activation(out=s_squared[:], in_=alive[("s", g, j)][:], func=ACT.Square)
-                alive[("s_squared", g, j)] = s_squared
+            for g in here([g]):
+                for j in range(GROUP_TILES):
+                    s_squared = work.tile([P, EXEMPLARS], F32, tag="s_squared", bufs=2 * GROUP_TILES)
+                    nc.scalar.activation(out=s_squared[:], in_=alive[("s", g, j)][:], func=ACT.Square)
+                    alive[("s_squared", g, j)] = s_squared
 
         def cube(g):
-            if absent(g):
-                return
-            for j in range(GROUP_TILES):
-                a = work.tile([P, EXEMPLARS], F32, tag="a", bufs=3 * GROUP_TILES)
-                nc.vector.tensor_tensor(out=a[:], in0=alive[("s", g, j)][:], in1=alive[("s_squared", g, j)][:], op=ALU.mult)
-                alive[("a", g, j)] = a
+            for g in here([g]):
+                a = work.tile([P, GROUP_TILES, EXEMPLARS], F32, tag="a", bufs=4)
+                for j in range(GROUP_TILES):
+                    nc.vector.tensor_tensor(
+                        out=a[:, j, :], in0=alive[("s", g, j)][:], in1=alive[("s_squared", g, j)][:], op=ALU.mult
+                    )
+                alive[("a", g)] = a
 
         def row_sums(g):
-            if absent(g):
-                return
-            sums = work.tile([P, GROUP_TILES], F32, tag="sums")
-            for j in range(GROUP_TILES):
-                if j == 1 and g % SCALAR_SUMS == 1:
-                    magnitudes = work.tile([P, EXEMPLARS], BF16, tag="magnitudes")
-                    nc.scalar.activation(
-                        out=magnitudes[:], in_=alive[("a", g, j)][:], func=ACT.Abs, accum_out=sums[:, j : j + 1]
-                    )
-                else:
+            for g in here([g]):
+                groups = sums_pair(g)
+                if g == groups[0]:
+                    sums = work.tile([P, len(groups) * GROUP_TILES], F32, tag="sums")
+                    alive[("sums", g)] = sums
+                first = groups.index(g) * GROUP_TILES
+                sums = alive[("sums", groups[0])][:, first : first + GROUP_TILES]
+                a = alive[("a", g)]
+                if g % 8 == 5 or g in (25, 27, 30, 31):
                     nc.vector.tensor_reduce(
-                        out=sums[:, j : j + 1], in_=alive[("a", g, j)][:], axis=AXES.X, op=ALU.add, apply_absolute_value=True
+                        out=sums[:, :1], in_=a[:, :1, :], axis=AXES.X, op=ALU.add, apply_absolute_value=True
                     )
-            alive[("sums", g)] = sums
+                    magnitudes = work.tile([P, EXEMPLARS], BF16, tag="magnitudes")
+                    nc.scalar.activation(out=magnitudes[:], in_=a[:, 1, :], func=ACT.Abs, accum_out=sums[:, 1:2])
+                else:
+                    nc.vector.tensor_reduce(out=sums, in_=a[:], axis=AXES.X, op=ALU.add, apply_absolute_value=True)
 
         def floor_sums(g):
-            if absent(g):
-                return
-            floored = work.tile([P, GROUP_TILES], F32, tag="floored")
-            nc.vector.tensor_scalar_max(out=floored[:], in0=alive[("sums", g)][:], scalar1=EPS)
-            alive[("floored", g)] = floored
+            for g in here([g]):
+                groups = sums_pair(g)
+                floored = work.tile([P, len(groups) * GROUP_TILES], F32, tag="floored")
+                nc.vector.tensor_scalar_max(out=floored[:], in0=alive[("sums", groups[0])][:], scalar1=EPS)
+                alive[("floored", groups[0])] = floored
 
         def invert_sums(g):
-            if absent(g):
-                return
-            inverse = work.tile([P, GROUP_TILES], F32, tag="inverse")
-            nc.vector.reciprocal(out=inverse[:], in_=alive[("floored", g)][:])
-            alive[("inverse", g)] = inverse
+            for g in here([g]):
+                groups = sums_pair(g)
+                inverse = work.tile([P, len(groups) * GROUP_TILES], F32, tag="inverse")
+                nc.vector.reciprocal(out=inverse[:], in_=alive[("floored", groups[0])][:])
+                alive[("inverse", groups[0])] = inverse
 
         def normalise(g):
-            if absent(g):
-                return
-            inverse = alive[("inverse", g)]
-            p = work.tile([P, GROUP_TILES, EXEMPLARS], BF16, tag="p", bufs=3)
-            for j in range(GROUP_TILES):
-                nc.gpsimd.tensor_scalar(
-                    out=p[:, j, :], in0=alive[("a", g, j)][:], scalar1=inverse[:, j : j + 1], scalar2=0.0,
-                    op0=ALU.mult, op1=ALU.add,
-                )
-            alive[("p", g)] = p
+            for g in here([g]):
+                groups = sums_pair(g)
+                inverse = alive[("inverse", groups[0])]
+                p = work.tile([P, GROUP_TILES, EXEMPLARS], BF16, tag="p", bufs=3)
+                for j in range(GROUP_TILES):
+                    i = groups.index(g) * GROUP_TILES + j
+                    a = alive[("a", g)][:, j, :]
+                    if g < N_GROUPS - VECTOR_LAST:
+                        nc.gpsimd.tensor_scalar(
+                            out=p[:, j, :], in0=a, scalar1=inverse[:, i : i + 1], scalar2=0.0, op0=ALU.mult, op1=ALU.add
+                        )
+                    else:
+                        nc.vector.tensor_scalar_mul(out=p[:, j, :], in0=a, scalar1=inverse[:, i : i + 1])
+                alive[("p", g)] = p
 
         def transpose_p(g):
-            if absent(g):
-                return
-            if g < N_GROUPS - BORROWERS:
-                bank = psum.tile([P, GROUP_TILES, 2, P], F32, tag="p_bank", bufs=1, name="p_bank")
-            else:
-                bank = psum.tile([P, GROUP_TILES, 2, P], F32, tag="s_bank", bufs=2 * GROUP_TILES, name="p_bank")
-            words = alive[("p", g)][:].rearrange("r j c -> r (j c)").bitcast(F32)
-            for j in range(GROUP_TILES):
-                for u in range(2):
-                    first = (2 * j + u) * P
-                    nc.tensor.transpose(bank[:, j, u, :], words[:, first : first + P], identity_f32[:])
-            alive[("p_bank", g)] = bank
+            for g in here([g]):
+                if g < N_GROUPS - BORROWERS:
+                    bank = psum.tile([P, GROUP_TILES, 2, P], F32, tag="p_bank", bufs=1, name="p_bank")
+                else:
+                    bank = psum.tile([P, GROUP_TILES, 2, P], F32, tag="s_bank", bufs=2 * GROUP_TILES, name="p_bank")
+                words = alive[("p", g)][:].rearrange("r j c -> r (j c)").bitcast(F32)
+                for j in range(GROUP_TILES):
+                    for u in range(2):
+                        first = (2 * j + u) * P
+                        nc.tensor.transpose(bank[:, j, u, :], words[:, first : first + P], identity_f32[:])
+                alive[("p_bank", g)] = bank
 
         def regroup_p(g):
-            if absent(g):
-                return
-            p_grouped = work.tile([P, GROUP_TILES * EXEMPLARS], BF16, tag="p_grouped", align_bytes=64)
-            grouped = p_grouped[:].bitcast(F32).rearrange("q (j r u) -> q j r u", j=GROUP_TILES, r=P, u=2)
-            nc.scalar.copy(out=grouped, in_=alive[("p_bank", g)][:].rearrange("q j u r -> q j r u"))
-            alive[("p_grouped", g)] = p_grouped
+            for g in here([g]):
+                groups = back_pair(g)
+                n = len(groups) * GROUP_TILES
+                if g == groups[0]:
+                    p_grouped = work.tile([P, n * EXEMPLARS], BF16, tag="p_grouped", align_bytes=64)
+                    alive[("p_grouped", g)] = p_grouped
+                grouped = alive[("p_grouped", groups[0])][:].bitcast(F32).rearrange("q (i r u) -> q i r u", i=n, r=P, u=2)
+                first = groups.index(g) * GROUP_TILES
+                nc.scalar.copy(
+                    out=grouped[:, first : first + GROUP_TILES], in_=alive[("p_bank", g)][:].rearrange("q j u r -> q j r u")
+                )
 
         def quantise_p(g):
-            if absent(g):
-                return
-            p_codes = work.tile([P, GROUP_TILES * P], U32, tag="p_codes", align_bytes=64)
-            p_scales = work.tile([P, GROUP_TILES * P], U8, tag="p_scales", align_bytes=64)
-            nc.vector.quantize_mx(
-                out=p_codes[:].bitcast(FP8X4),
-                scales=p_scales[:],
-                in_=alive[("p_grouped", g)][:],
-            )
-            alive[("p_codes", g)] = (p_codes, p_scales)
+            for g in here([g]):
+                n = len(back_pair(g)) * GROUP_TILES * P
+                p_codes = work.tile([P, n], U32, tag="p_codes", align_bytes=64)
+                p_scales = work.tile([P, n], U8, tag="p_scales", align_bytes=64)
+                nc.vector.quantize_mx(out=p_codes[:].bitcast(FP8X4), scales=p_scales[:], in_=alive[("p_grouped", g)][:])
+                alive[("p_codes", g)] = (p_codes, p_scales)
 
         def read_out(g):
-            if absent(g):
-                return
-            p_codes, p_scales = alive[("p_codes", g)]
-            if g < N_GROUPS - BORROWERS:
-                echo = psum.tile([P, GROUP_TILES, LABELS], F32, tag="echo_bank", bufs=1, name="echo")
-            else:
-                echo = psum.tile([P, GROUP_TILES, LABELS], F32, tag="f_bank", bufs=GROUP_TILES, name="echo")
-            for j in range(GROUP_TILES):
-                nc.tensor.matmul_mx(
-                    out=echo[:, j, :],
-                    lhsT=p_codes[:, j * P : (j + 1) * P].bitcast(FP8X4),
-                    lhsT_scale=p_scales[:, j * P : (j + 1) * P],
-                    rhs=r_codes[:].bitcast(FP8X4),
-                    rhs_scale=r_scales[:],
-                    start=True,
-                    stop=True,
-                )
-            alive[("echo", g)] = echo
+            for g in here([g]):
+                n = len(back_pair(g)) * GROUP_TILES
+                p_codes, p_scales = alive[("p_codes", g)]
+                if g < N_GROUPS - BORROWERS:
+                    echo = psum.tile([P, n, LABELS], F32, tag="echo_bank", bufs=1, name="echo")
+                else:
+                    echo = psum.tile([P, n, LABELS], F32, tag="f_bank", bufs=2, name="echo")
+                for i in range(n):
+                    nc.tensor.matmul_mx(
+                        out=echo[:, i, :],
+                        lhsT=p_codes[:, i * P : (i + 1) * P].bitcast(FP8X4),
+                        lhsT_scale=p_scales[:, i * P : (i + 1) * P],
+                        rhs=r_codes[:].bitcast(FP8X4),
+                        rhs_scale=r_scales[:],
+                        start=True,
+                        stop=True,
+                    )
+                alive[("echo", g)] = echo
 
         def store(g):
-            if absent(g):
-                return
-            echo_rows = work.tile([P, GROUP_TILES, LABELS], F32, tag="echo_rows", bufs=8)
-            nc.scalar.copy(out=echo_rows[:], in_=alive[("echo", g)][:])
-            c = g * GROUP_TILES // CHUNK_TILES
-            first_tile = g * GROUP_TILES % CHUNK_TILES
-            rows = out[c * P * CHUNK_TILES : (c + 1) * P * CHUNK_TILES, :].rearrange("(p t) l -> p t l", t=CHUNK_TILES)
-            nc.sync.dma_start(out=rows[:, first_tile : first_tile + GROUP_TILES, :], in_=echo_rows[:])
+            for g in here([g]):
+                n = len(back_pair(g)) * GROUP_TILES
+                echo_rows = work.tile([P, n, LABELS], F32, tag="echo_rows", bufs=4)
+                nc.scalar.copy(out=echo_rows[:], in_=alive[("echo", g)][:])
+                c = g * GROUP_TILES // CHUNK_TILES
+                first_tile = g * GROUP_TILES % CHUNK_TILES
+                rows = out[c * P * CHUNK_TILES : (c + 1) * P * CHUNK_TILES, :].rearrange("(p t) l -> p t l", t=CHUNK_TILES)
+                nc.sync.dma_start(out=rows[:, first_tile : first_tile + n, :], in_=echo_rows[:])
 
-        transpose_f(0)
-        regroup_f(0)
+        transpose_f(0, 0)
+        transpose_f(0, 1)
+        regroup_f(0, 0)
+        regroup_f(0, 1)
         transpose_e()
         quantise_f(0)
         quantise_e()
         quantise_r()
-        transpose_f(1)
+        transpose_f(1, 0)
+        transpose_f(1, 1)
+        regroup_f(1, 0)
+        regroup_f(1, 1)
+        quantise_f(1)
+        transpose_f(2, 0)
+        transpose_f(2, 1)
+        regroup_f(2, 0)
+        regroup_f(2, 1)
+        transpose_f(3, 0)
+        transpose_f(3, 1)
 
-        for period in range(-1, N_GROUPS + 5):
-            quantise_p(period - 4)
-            transpose_p(period - 3)
-            regroup_f(period + 2)
-            similarities(period)
-            invert_sums(period - 2)
-            normalise(period - 2)
-            cube(period - 1)
-            store(period - 5)
-            regroup_p(period - 3)
-            square(period)
-            read_out(period - 4)
-            row_sums(period - 1)
-            transpose_f(period + 3)
-            quantise_f(period + 2)
-            floor_sums(period - 1)
+        for b in range(-2, N_GROUPS - 2, 2):
+            normalise(b - 3)
+            normalise(b - 2)
+            read_out(b - 6)
+            regroup_f(b + 5, 0)
+            regroup_p(b - 4)
+            regroup_f(b + 5, 1)
+            store(b - 6)
+            cube(b)
+            similarities(b + 2)
+            row_sums(b - 1)
+            square(b + 2)
+            transpose_p(b - 3)
+            transpose_f(b + 6, 0)
+            transpose_f(b + 6, 1)
+            regroup_f(b + 6, 0)
+            regroup_p(b - 3)
+            regroup_f(b + 6, 1)
+            cube(b + 1)
+            similarities(b + 3)
+            square(b + 3)
+            transpose_p(b - 2)
+            transpose_f(b + 7, 0)
+            transpose_f(b + 7, 1)
+            row_sums(b)
+            quantise_f(b + 4)
+            floor_sums(b)
+            quantise_p(b - 4)
+            invert_sums(b)
+
+        normalise(27)
+        normalise(28)
+        cube(30)
+        read_out(24)
+        regroup_p(26)
+        row_sums(29)
+        store(24)
+        transpose_p(27)
+        regroup_p(27)
+        cube(31)
+        row_sums(30)
+        transpose_p(28)
+        regroup_p(28)
+        row_sums(31)
+        floor_sums(30)
+        quantise_p(26)
+        invert_sums(30)
+        floor_sums(31)
+        normalise(29)
+        normalise(30)
+        invert_sums(31)
+        read_out(26)
+        store(26)
+        transpose_p(29)
+        regroup_p(29)
+        transpose_p(30)
+        regroup_p(30)
+        normalise(31)
+        quantise_p(28)
+        transpose_p(31)
+        regroup_p(31)
+        read_out(28)
+        store(28)
+        quantise_p(30)
+        read_out(30)
+        store(30)
+        quantise_p(31)
+        read_out(31)
+        store(31)

@@ -64,9 +64,9 @@ def tile_minerva_pa_t_kernel(tc, f_norm, e_norm, ex_class_reps, out):
             )
         for t in range(GROUP_TILES, CHUNK_TILES):
             load_f(0, t, t + 1)
+        for t in range(CHUNK_TILES):
+            load_f(1, t, t + 1)
         nc.sync.dma_start(out=r_rows[:], in_=ex_class_reps.rearrange("(u q e) l -> q u e l", u=2, e=2))
-        load_f(1, 0, GROUP_TILES)
-        load_f(1, GROUP_TILES, CHUNK_TILES)
         for c in range(2, N_CHUNKS):
             load_f(c, 0, CHUNK_TILES)
 
@@ -83,16 +83,15 @@ def tile_minerva_pa_t_kernel(tc, f_norm, e_norm, ex_class_reps, out):
         e_codes = const.tile([P, F_PASSES * EXEMPLARS], U32, align_bytes=64)
         e_scales = const.tile([P, F_PASSES * EXEMPLARS], U8, align_bytes=64)
 
-        def transpose_e():
+        def transpose_e(j):
             e_pairs = e_rows[:].bitcast(F32)
             grouped = e_grouped[:].bitcast(F32).rearrange("q (h j r u) -> q h j r u", h=F_PASSES, j=PACK, r=P, u=2)
-            for j in range(PACK):
-                bank = psum.tile([P, F_PASSES, 2, P], F32, tag="s_bank", bufs=2 * GROUP_TILES, name="e_bank")
-                transpose_pairs(bank, e_pairs[:, j * FEATURES // 2 : (j + 1) * FEATURES // 2])
-                if j % 2 == 0:
-                    nc.scalar.copy(out=grouped[:, :, j, :, :], in_=pairs_side_by_side(bank))
-                else:
-                    nc.vector.tensor_copy(out=grouped[:, :, j, :, :], in_=pairs_side_by_side(bank))
+            bank = psum.tile([P, F_PASSES, 2, P], F32, tag="s_bank", bufs=2 * GROUP_TILES, name="e_bank")
+            transpose_pairs(bank, e_pairs[:, j * FEATURES // 2 : (j + 1) * FEATURES // 2])
+            if j % 2 == 0:
+                nc.scalar.copy(out=grouped[:, :, j, :, :], in_=pairs_side_by_side(bank))
+            else:
+                nc.vector.tensor_copy(out=grouped[:, :, j, :, :], in_=pairs_side_by_side(bank))
 
         def quantise_e():
             for h in range(F_PASSES):
@@ -106,8 +105,10 @@ def tile_minerva_pa_t_kernel(tc, f_norm, e_norm, ex_class_reps, out):
         r_codes = const.tile([P, LABELS], U32, align_bytes=64)
         r_scales = const.tile([P, LABELS], U8, align_bytes=64)
 
-        def quantise_r():
+        def group_r():
             nc.vector.tensor_copy(out=r_grouped[:], in_=r_rows[:].rearrange("q u e l -> q l (u e)"))
+
+        def quantise_r():
             nc.vector.quantize_mx(
                 out=r_codes[:].bitcast(FP8X4), scales=r_scales[:], in_=r_grouped[:].rearrange("q l t -> q (l t)")
             )
@@ -312,31 +313,43 @@ def tile_minerva_pa_t_kernel(tc, f_norm, e_norm, ex_class_reps, out):
         transpose_f(0, 1)
         regroup_f(0, 0)
         regroup_f(0, 1)
-        transpose_e()
+        transpose_e(0)
+        transpose_e(1)
         quantise_f(0)
-        quantise_e()
-        quantise_r()
+        transpose_e(2)
+        transpose_e(3)
         transpose_f(1, 0)
         transpose_f(1, 1)
         regroup_f(1, 0)
         regroup_f(1, 1)
+        quantise_e()
         quantise_f(1)
         transpose_f(2, 0)
         transpose_f(2, 1)
         regroup_f(2, 0)
         regroup_f(2, 1)
+        similarities(0)
+        square(0)
         transpose_f(3, 0)
         transpose_f(3, 1)
+        group_r()
+        regroup_f(3, 0)
+        regroup_f(3, 1)
+        similarities(1)
+        quantise_r()
+        cube(0)
+        square(1)
+        transpose_f(4, 0)
+        transpose_f(4, 1)
+        regroup_f(4, 0)
+        regroup_f(4, 1)
+        quantise_f(2)
+        transpose_f(5, 0)
+        transpose_f(5, 1)
+        regroup_f(5, 0)
+        regroup_f(5, 1)
 
-        for b in range(-2, N_GROUPS - 2, 2):
-            normalise(b - 3)
-            normalise(b - 2)
-            read_out(b - 6)
-            regroup_f(b + 5, 0)
-            regroup_p(b - 4)
-            regroup_f(b + 5, 1)
-            store(b - 6)
-            cube(b)
+        for b in range(0, N_GROUPS - 2, 2):
             similarities(b + 2)
             row_sums(b - 1)
             square(b + 2)
@@ -357,35 +370,37 @@ def tile_minerva_pa_t_kernel(tc, f_norm, e_norm, ex_class_reps, out):
             floor_sums(b)
             quantise_p(b - 4)
             invert_sums(b)
+            normalise(b - 1)
+            normalise(b)
+            read_out(b - 4)
+            regroup_f(b + 7, 0)
+            regroup_p(b - 2)
+            regroup_f(b + 7, 1)
+            store(b - 4)
+            cube(b + 2)
 
-        normalise(27)
-        normalise(28)
-        cube(30)
-        read_out(24)
-        regroup_p(26)
         row_sums(29)
-        store(24)
-        transpose_p(27)
-        regroup_p(27)
         cube(31)
         row_sums(30)
+        transpose_p(27)
+        regroup_p(27)
+        row_sums(31)
         transpose_p(28)
         regroup_p(28)
-        row_sums(31)
         floor_sums(30)
+        floor_sums(31)
         quantise_p(26)
         invert_sums(30)
-        floor_sums(31)
+        invert_sums(31)
         normalise(29)
         normalise(30)
-        invert_sums(31)
+        normalise(31)
         read_out(26)
         store(26)
         transpose_p(29)
         regroup_p(29)
         transpose_p(30)
         regroup_p(30)
-        normalise(31)
         quantise_p(28)
         transpose_p(31)
         regroup_p(31)

from contextlib import ExitStack

import concourse.mybir as mybir
from concourse.masks import make_identity

F32 = mybir.dt.float32
BF16 = mybir.dt.bfloat16
U32 = mybir.dt.uint32
U8 = mybir.dt.uint8
FP8X4 = mybir.dt.float8_e4m3fn_x4
ALU = mybir.AluOpType
ACT = mybir.ActivationFunctionType
AXES = mybir.AxisListType

P = 128
ROWS, FEATURES, EXEMPLARS, LABELS = 8192, 1024, 512, 128
EPS = 1e-12
FLOPS = 2 * ROWS * FEATURES * EXEMPLARS + 2 * ROWS * EXEMPLARS * LABELS

PACK = 4
F_PASSES = FEATURES // (P * PACK)
CHUNK_TILES = 4
N_CHUNKS = ROWS // (P * CHUNK_TILES)
GROUP_TILES = 2
N_GROUPS = ROWS // (P * GROUP_TILES)
BORROWERS = 3
SINGLE_FRONT = 2
SINGLE_BACK = N_GROUPS - 2
VECTOR_LAST = 3


def tile_minerva_pa_t_kernel(tc, f_norm, e_norm, ex_class_reps, out):
    nc = tc.nc
    with ExitStack() as ctx:
        const = ctx.enter_context(tc.tile_pool(name="const", bufs=1))
        loads = ctx.enter_context(tc.tile_pool(name="loads", bufs=N_CHUNKS))
        work = ctx.enter_context(tc.tile_pool(name="work", bufs=2))
        psum = ctx.enter_context(tc.psum_pool(name="psum", bufs=1))
        ctx.enter_context(tc.manual_schedule())

        identity_f32 = const.tile([P, P], F32)
        make_identity(nc, identity_f32[:])

        f_chunks = []
        for c in range(N_CHUNKS):
            f_chunk = loads.tile([P, CHUNK_TILES * FEATURES], BF16, tag="f_chunk")
            f_chunks.append(f_chunk)
        e_rows = const.tile([P, PACK * FEATURES], BF16)
        r_rows = const.tile([P, 2, 2, LABELS], BF16)

        def load_f(c, first_tile, end_tile):
            rows = f_norm[c * P * CHUNK_TILES : (c + 1) * P * CHUNK_TILES, :].rearrange("(p t) k -> p t k", t=CHUNK_TILES)
            nc.sync.dma_start(
                out=f_chunks[c][:, first_tile * FEATURES : end_tile * FEATURES],
                in_=rows[:, first_tile:end_tile, :].rearrange("p t k -> p (t k)"),
            )

        for t in range(GROUP_TILES):
            load_f(0, t, t + 1)
        for j in range(PACK):
            nc.sync.dma_start(
                out=e_rows[:, j * FEATURES : (j + 1) * FEATURES],
                in_=e_norm[j * P : (j + 1) * P, :],
            )
        for t in range(GROUP_TILES, CHUNK_TILES):
            load_f(0, t, t + 1)
        for t in range(CHUNK_TILES):
            load_f(1, t, t + 1)
        nc.sync.dma_start(out=r_rows[:], in_=ex_class_reps.rearrange("(u q e) l -> q u e l", u=2, e=2))
        for c in range(2, N_CHUNKS):
            load_f(c, 0, CHUNK_TILES)

        def transpose_pairs(bank, pairs):
            for h in range(F_PASSES):
                for u in range(2):
                    first = (2 * h + u) * P
                    nc.tensor.transpose(bank[:, h, u, :], pairs[:, first : first + P], identity_f32[:])

        def pairs_side_by_side(bank):
            return bank[:].rearrange("q h u r -> q h r u")

        e_grouped = const.tile([P, F_PASSES * EXEMPLARS * PACK], BF16, align_bytes=64)
        e_codes = const.tile([P, F_PASSES * EXEMPLARS], U32, align_bytes=64)
        e_scales = const.tile([P, F_PASSES * EXEMPLARS], U8, align_bytes=64)

        def transpose_e(j):
            e_pairs = e_rows[:].bitcast(F32)
            grouped = e_grouped[:].bitcast(F32).rearrange("q (h j r u) -> q h j r u", h=F_PASSES, j=PACK, r=P, u=2)
            bank = psum.tile([P, F_PASSES, 2, P], F32, tag="s_bank", bufs=2 * GROUP_TILES, name="e_bank")
            transpose_pairs(bank, e_pairs[:, j * FEATURES // 2 : (j + 1) * FEATURES // 2])
            if j % 2 == 0:
                nc.scalar.copy(out=grouped[:, :, j, :, :], in_=pairs_side_by_side(bank))
            else:
                nc.vector.tensor_copy(out=grouped[:, :, j, :, :], in_=pairs_side_by_side(bank))

        def quantise_e():
            for h in range(F_PASSES):
                nc.vector.quantize_mx(
                    out=e_codes[:, h * EXEMPLARS : (h + 1) * EXEMPLARS].bitcast(FP8X4),
                    scales=e_scales[:, h * EXEMPLARS : (h + 1) * EXEMPLARS],
                    in_=e_grouped[:, h * EXEMPLARS * PACK : (h + 1) * EXEMPLARS * PACK],
                )

        r_grouped = const.tile([P, LABELS, PACK], BF16, align_bytes=64)
        r_codes = const.tile([P, LABELS], U32, align_bytes=64)
        r_scales = const.tile([P, LABELS], U8, align_bytes=64)

        def group_r():
            nc.vector.tensor_copy(out=r_grouped[:], in_=r_rows[:].rearrange("q u e l -> q l (u e)"))

        def quantise_r():
            nc.vector.quantize_mx(
                out=r_codes[:].bitcast(FP8X4), scales=r_scales[:], in_=r_grouped[:].rearrange("q l t -> q (l t)")
            )

        alive = {}

        def here(groups):
            return [g for g in groups if 0 <= g < N_GROUPS]

        def front_pair(g):
            return [g] if g < SINGLE_FRONT else [g - g % 2, g - g % 2 + 1]

        def sums_pair(g):
            return here([g - 1, g] if g % 2 == 0 else [g, g + 1])

        def back_pair(g):
            return [g] if g >= SINGLE_BACK else [g - g % 2, g - g % 2 + 1]

        def transpose_f(g, j):
            for g in here([g]):
                t = g * GROUP_TILES + j
                pairs = f_chunks[t // CHUNK_TILES][:].bitcast(F32)
                first = (t % CHUNK_TILES) * FEATURES // 2
                bank = psum.tile([P, F_PASSES, 2, P], F32, tag="f_bank", bufs=2, name="f_bank")
                transpose_pairs(bank, pairs[:, first : first + FEATURES // 2])
                alive[("f_bank", g, j)] = bank

        def regroup_f(g, j):
            for g in here([g]):
                groups = front_pair(g)
                n = len(groups) * GROUP_TILES
                if g == groups[0] and j == 0:
                    f_grouped = work.tile([P, n * FEATURES], BF16, tag="f_grouped", align_bytes=64)
                    alive[("f_grouped", g)] = f_grouped
                f_grouped = alive[("f_grouped", groups[0])]
                grouped = f_grouped[:].bitcast(F32).rearrange("q (i h r u) -> q i h r u", i=n, h=F_PASSES, r=P, u=2)
                i = groups.index(g) * GROUP_TILES + j
                words = pairs_side_by_side(alive[("f_bank", g, j)])
                if g == 0 and j == 1:
                    nc.vector.tensor_copy(out=grouped[:, i], in_=words)
                else:
                    nc.scalar.copy(out=grouped[:, i], in_=words)

        def quantise_f(g):
            for g in here([g]):
                n = len(front_pair(g)) * GROUP_TILES * F_PASSES * P
                f_codes = work.tile([P, n], U32, tag="f_codes", bufs=3, align_bytes=64)
                f_scales = work.tile([P, n], U8, tag="f_scales", bufs=3, align_bytes=64)
                nc.vector.quantize_mx(out=f_codes[:].bitcast(FP8X4), scales=f_scales[:], in_=alive[("f_grouped", g)][:])
                alive[("f_codes", g)] = (f_codes, f_scales)

        def similarities(g):
            for g in here([g]):
                groups = front_pair(g)
                f_codes, f_scales = alive[("f_codes", groups[0])]
                for j in range(GROUP_TILES):
                    s = psum.tile([P, EXEMPLARS], F32, tag="s_bank", bufs=2 * GROUP_TILES, name="s")
                    for h in range(F_PASSES):
                        k = (groups.index(g) * GROUP_TILES + j) * F_PASSES + h
                        rows = slice(k * P, (k + 1) * P)
                        exemplars = slice(h * EXEMPLARS, (h + 1) * EXEMPLARS)
                        nc.tensor.matmul_mx(
                            out=s[:],
                            lhsT=f_codes[:, rows].bitcast(FP8X4),
                            lhsT_scale=f_scales[:, rows],
                            rhs=e_codes[:, exemplars].bitcast(FP8X4),
                            rhs_scale=e_scales[:, exemplars],
                            start=(h == 0),
                            stop=(h == F_PASSES - 1),
                        )
                    alive[("s", g, j)] = s

        def square(g):
            for g in here([g]):
                for j in range(GROUP_TILES):
                    s_squared = work.tile([P, EXEMPLARS], F32, tag="s_squared", bufs=2 * GROUP_TILES)
                    nc.scalar.activation(out=s_squared[:], in_=alive[("s", g, j)][:], func=ACT.Square)
                    alive[("s_squared", g, j)] = s_squared

        def cube(g):
            for g in here([g]):
                a = work.tile([P, GROUP_TILES, EXEMPLARS], F32, tag="a", bufs=4)
                for j in range(GROUP_TILES):
                    nc.vector.tensor_tensor(
                        out=a[:, j, :], in0=alive[("s", g, j)][:], in1=alive[("s_squared", g, j)][:], op=ALU.mult
                    )
                alive[("a", g)] = a

        def row_sums(g):
            for g in here([g]):
                groups = sums_pair(g)
                if g == groups[0]:
                    sums = work.tile([P, len(groups) * GROUP_TILES], F32, tag="sums")
                    alive[("sums", g)] = sums
                first = groups.index(g) * GROUP_TILES
                sums = alive[("sums", groups[0])][:, first : first + GROUP_TILES]
                a = alive[("a", g)]
                if g % 8 == 5 or g in (25, 27, 30, 31):
                    nc.vector.tensor_reduce(
                        out=sums[:, :1], in_=a[:, :1, :], axis=AXES.X, op=ALU.add, apply_absolute_value=True
                    )
                    magnitudes = work.tile([P, EXEMPLARS], BF16, tag="magnitudes")
                    nc.scalar.activation(out=magnitudes[:], in_=a[:, 1, :], func=ACT.Abs, accum_out=sums[:, 1:2])
                else:
                    nc.vector.tensor_reduce(out=sums, in_=a[:], axis=AXES.X, op=ALU.add, apply_absolute_value=True)

        def floor_sums(g):
            for g in here([g]):
                groups = sums_pair(g)
                floored = work.tile([P, len(groups) * GROUP_TILES], F32, tag="floored")
                nc.vector.tensor_scalar_max(out=floored[:], in0=alive[("sums", groups[0])][:], scalar1=EPS)
                alive[("floored", groups[0])] = floored

        def invert_sums(g):
            for g in here([g]):
                groups = sums_pair(g)
                inverse = work.tile([P, len(groups) * GROUP_TILES], F32, tag="inverse")
                nc.vector.reciprocal(out=inverse[:], in_=alive[("floored", groups[0])][:])
                alive[("inverse", groups[0])] = inverse

        def normalise(g):
            for g in here([g]):
                groups = sums_pair(g)
                inverse = alive[("inverse", groups[0])]
                p = work.tile([P, GROUP_TILES, EXEMPLARS], BF16, tag="p", bufs=3)
                for j in range(GROUP_TILES):
                    i = groups.index(g) * GROUP_TILES + j
                    a = alive[("a", g)][:, j, :]
                    if g < N_GROUPS - VECTOR_LAST:
                        nc.gpsimd.tensor_scalar(
                            out=p[:, j, :], in0=a, scalar1=inverse[:, i : i + 1], scalar2=0.0, op0=ALU.mult, op1=ALU.add
                        )
                    else:
                        nc.vector.tensor_scalar_mul(out=p[:, j, :], in0=a, scalar1=inverse[:, i : i + 1])
                alive[("p", g)] = p

        def transpose_p(g):
            for g in here([g]):
                if g < N_GROUPS - BORROWERS:
                    bank = psum.tile([P, GROUP_TILES, 2, P], F32, tag="p_bank", bufs=1, name="p_bank")
                else:
                    bank = psum.tile([P, GROUP_TILES, 2, P], F32, tag="s_bank", bufs=2 * GROUP_TILES, name="p_bank")
                words = alive[("p", g)][:].rearrange("r j c -> r (j c)").bitcast(F32)
                for j in range(GROUP_TILES):
                    for u in range(2):
                        first = (2 * j + u) * P
                        nc.tensor.transpose(bank[:, j, u, :], words[:, first : first + P], identity_f32[:])
                alive[("p_bank", g)] = bank

        def regroup_p(g):
            for g in here([g]):
                groups = back_pair(g)
                n = len(groups) * GROUP_TILES
                if g == groups[0]:
                    p_grouped = work.tile([P, n * EXEMPLARS], BF16, tag="p_grouped", align_bytes=64)
                    alive[("p_grouped", g)] = p_grouped
                grouped = alive[("p_grouped", groups[0])][:].bitcast(F32).rearrange("q (i r u) -> q i r u", i=n, r=P, u=2)
                first = groups.index(g) * GROUP_TILES
                nc.scalar.copy(
                    out=grouped[:, first : first + GROUP_TILES], in_=alive[("p_bank", g)][:].rearrange("q j u r -> q j r u")
                )

        def quantise_p(g):
            for g in here([g]):
                n = len(back_pair(g)) * GROUP_TILES * P
                p_codes = work.tile([P, n], U32, tag="p_codes", align_bytes=64)
                p_scales = work.tile([P, n], U8, tag="p_scales", align_bytes=64)
                nc.vector.quantize_mx(out=p_codes[:].bitcast(FP8X4), scales=p_scales[:], in_=alive[("p_grouped", g)][:])
                alive[("p_codes", g)] = (p_codes, p_scales)

        def read_out(g):
            for g in here([g]):
                n = len(back_pair(g)) * GROUP_TILES
                p_codes, p_scales = alive[("p_codes", g)]
                if g < N_GROUPS - BORROWERS:
                    echo = psum.tile([P, n, LABELS], F32, tag="echo_bank", bufs=1, name="echo")
                else:
                    echo = psum.tile([P, n, LABELS], F32, tag="f_bank", bufs=2, name="echo")
                for i in range(n):
                    nc.tensor.matmul_mx(
                        out=echo[:, i, :],
                        lhsT=p_codes[:, i * P : (i + 1) * P].bitcast(FP8X4),
                        lhsT_scale=p_scales[:, i * P : (i + 1) * P],
                        rhs=r_codes[:].bitcast(FP8X4),
                        rhs_scale=r_scales[:],
                        start=True,
                        stop=True,
                    )
                alive[("echo", g)] = echo

        def store(g):
            for g in here([g]):
                n = len(back_pair(g)) * GROUP_TILES
                echo_rows = work.tile([P, n, LABELS], F32, tag="echo_rows", bufs=4)
                nc.scalar.copy(out=echo_rows[:], in_=alive[("echo", g)][:])
                c = g * GROUP_TILES // CHUNK_TILES
                first_tile = g * GROUP_TILES % CHUNK_TILES
                rows = out[c * P * CHUNK_TILES : (c + 1) * P * CHUNK_TILES, :].rearrange("(p t) l -> p t l", t=CHUNK_TILES)
                nc.sync.dma_start(out=rows[:, first_tile : first_tile + n, :], in_=echo_rows[:])

        transpose_f(0, 0)
        transpose_f(0, 1)
        regroup_f(0, 0)
        regroup_f(0, 1)
        transpose_e(0)
        transpose_e(1)
        quantise_f(0)
        transpose_e(2)
        transpose_e(3)
        transpose_f(1, 0)
        transpose_f(1, 1)
        regroup_f(1, 0)
        regroup_f(1, 1)
        quantise_e()
        quantise_f(1)
        transpose_f(2, 0)
        transpose_f(2, 1)
        regroup_f(2, 0)
        regroup_f(2, 1)
        similarities(0)
        square(0)
        transpose_f(3, 0)
        transpose_f(3, 1)
        group_r()
        regroup_f(3, 0)
        regroup_f(3, 1)
        similarities(1)
        quantise_r()
        cube(0)
        square(1)
        transpose_f(4, 0)
        transpose_f(4, 1)
        regroup_f(4, 0)
        regroup_f(4, 1)
        quantise_f(2)
        transpose_f(5, 0)
        transpose_f(5, 1)
        regroup_f(5, 0)
        regroup_f(5, 1)

        for b in range(0, N_GROUPS - 2, 2):
            similarities(b + 2)
            row_sums(b - 1)
            square(b + 2)
            transpose_p(b - 3)
            transpose_f(b + 6, 0)
            transpose_f(b + 6, 1)
            regroup_f(b + 6, 0)
            regroup_p(b - 3)
            regroup_f(b + 6, 1)
            cube(b + 1)
            similarities(b + 3)
            square(b + 3)
            transpose_p(b - 2)
            transpose_f(b + 7, 0)
            transpose_f(b + 7, 1)
            row_sums(b)
            quantise_f(b + 4)
            floor_sums(b)
            quantise_p(b - 4)
            invert_sums(b)
            normalise(b - 1)
            normalise(b)
            read_out(b - 4)
            regroup_f(b + 7, 0)
            regroup_p(b - 2)
            regroup_f(b + 7, 1)
            store(b - 4)
            cube(b + 2)

        row_sums(29)
        cube(31)
        row_sums(30)
        transpose_p(27)
        regroup_p(27)
        row_sums(31)
        transpose_p(28)
        regroup_p(28)
        floor_sums(30)
        floor_sums(31)
        quantise_p(26)
        invert_sums(30)
        invert_sums(31)
        normalise(29)
        normalise(30)
        normalise(31)
        read_out(26)
        store(26)
        transpose_p(29)
        regroup_p(29)
        transpose_p(30)
        regroup_p(30)
        quantise_p(28)
        transpose_p(31)
        regroup_p(31)
        read_out(28)
        store(28)
        quantise_p(30)
        read_out(30)
        store(30)
        quantise_p(31)
        read_out(31)
        store(31)
